import numpy as np
import ml_dtypes


def mxq(x, axis, fmt="e4m3"):
    dtype, down = {"e4m3": (ml_dtypes.float8_e4m3fn, 7), "e5m2": (ml_dtypes.float8_e5m2, 14)}[fmt]
    v = np.moveaxis(np.asarray(x, np.float32).astype(ml_dtypes.bfloat16).astype(np.float64), axis, -1)
    blocks = v.reshape(v.shape[:-1] + (-1, 32))
    amax = np.abs(blocks).max(-1, keepdims=True)
    byte = np.maximum(np.where(amax > 0, np.frexp(amax)[1] - 1 + 127, 0) - down, 1)
    scale = np.exp2(byte - 127.0)
    codes = (blocks / scale).astype(np.float32).astype(dtype).astype(np.float64)
    return np.moveaxis((codes * scale).reshape(v.shape), -1, axis)


WIDE = False


def mx_kscale(k):
    if not WIDE:
        return np.ones(k)
    levels = np.array([10, -10, 5, -5, 0])
    a = np.random.permutation(np.resize(levels, k // 512 * 4)).reshape(k // 512, 4)
    idx = np.arange(k)
    return np.exp2(a[idx // 512, idx % 128 // 32])


BF16 = ml_dtypes.bfloat16


def bf(x):
    return np.asarray(x, np.float32).astype(BF16)


def f64(x):
    return np.asarray(x).astype(np.float64)


B, N, C, E = 2, 512, 1024, 1024
EPS_NORM = 1e-12


def setup_inputs():
    t = mx_kscale(E)
    g = np.random.standard_normal((B, N, E)) ** 2
    cm = np.sqrt((1.0 + 0.01 * N) / 3.0)
    kv = 0.8 * np.random.standard_normal((B, E, E)) + cm * np.random.standard_normal((B, 1, E))
    return {"q_feat": bf(g / g.sum(axis=2, keepdims=True)),
            "kv": bf(kv * t),
            "v": bf(np.random.standard_normal((B, N, E)) * t),
            "w_proj": bf(np.random.standard_normal((E, C)) / np.sqrt(E) / t[:, None]),
            "b_proj": bf(0.2 * np.random.standard_normal(C))}


def reference(q_feat, kv, v, w_proj, b_proj):
    qf = f64(q_feat)
    nrm = np.sqrt((qf * qf).sum(axis=2, keepdims=True))
    q2 = qf / np.maximum(nrm, EPS_NORM)
    t2 = (mxq(q2, 2, "e4m3") @ mxq(f64(kv), 1, "e4m3")) / np.sqrt(N)
    h = f64(v) + t2
    return (mxq(h, 2, "e4m3") @ mxq(f64(w_proj), 0, "e4m3")) + f64(b_proj)

@@ -1,0 +1,284 @@
+import math
+from contextlib import ExitStack
+
+import concourse.mybir as mybir
+from concourse.masks import make_identity
+
+BF16 = mybir.dt.bfloat16
+F32 = mybir.dt.float32
+U32 = mybir.dt.uint32
+U8 = mybir.dt.uint8
+FP8X4 = mybir.dt.float8_e4m3fn_x4
+ALU = mybir.AluOpType
+ACT = mybir.ActivationFunctionType
+
+P = 128
+BATCH = 2
+TOKENS = 512
+FEAT = 1024
+OUT_COLS = 1024
+EPS_NORM = 1e-12
+
+SLOTS = 4
+HALVES = 2
+PASSES = FEAT // (P * SLOTS)
+TILES = TOKENS // P
+ALL_TILES = BATCH * TILES
+BANK = 512
+
+KV_ON_SCALAR = (1, 2)
+W_ON_SCALAR = (2, 2)
+
+FLOPS = 2 * BATCH * TOKENS * FEAT * FEAT + 2 * BATCH * TOKENS * FEAT * OUT_COLS
+
+
+def tile_essattn_pb_kernel(tc, q_feat, kv, v, w_proj, b_proj, out):
+    nc = tc.nc
+    with ExitStack() as ctx:
+        const = ctx.enter_context(tc.tile_pool(name="const", bufs=1))
+        inputs = ctx.enter_context(tc.tile_pool(name="inputs", bufs=1))
+        keep = ctx.enter_context(tc.tile_pool(name="keep", bufs=1))
+        scratch = ctx.enter_context(tc.tile_pool(name="scratch", bufs=2))
+        regroup_pool = ctx.enter_context(tc.tile_pool(name="regroup", bufs=5))
+        h_pool = ctx.enter_context(tc.tile_pool(name="h", bufs=4))
+        store_pool = ctx.enter_context(tc.tile_pool(name="store", bufs=8))
+        psum = ctx.enter_context(tc.psum_pool(name="psum", bufs=8))
+
+        one = const.tile([P, 1], F32)
+        nc.vector.memset(one[:], 1.0)
+        table_warm = const.tile([P, 1], F32)
+        nc.scalar.sqrt(out=table_warm[:], in_=one[:])
+        ident = const.tile([P, P], F32)
+        make_identity(nc, ident[:])
+
+        q_sb = [inputs.tile([P, TILES, FEAT], BF16, name="q_sb%d" % b) for b in range(BATCH)]
+        v_sb = [inputs.tile([P, TILES, FEAT], BF16, name="v_sb%d" % b) for b in range(BATCH)]
+        kv_sb = [
+            [inputs.tile([P, SLOTS, FEAT], BF16, name="kv_sb%d%d" % (b, c)) for c in range(PASSES)]
+            for b in range(BATCH)
+        ]
+        w_sb = [inputs.tile([P, SLOTS, OUT_COLS], BF16, name="w_sb%d" % g) for g in range(PASSES)]
+        bias_bc = const.tile([P, OUT_COLS], BF16)
+
+        for b in range(BATCH):
+            q_rows = q_feat[b].rearrange("(i p) k -> p i k", p=P)
+            kv_rows = kv[b].rearrange(
+                "(c u p e) n -> c p u (e n)", c=PASSES, u=HALVES, p=P, e=2
+            )
+            for c in range(PASSES):
+                pair = slice(2 * c, 2 * c + 2)
+                nc.sync.dma_start(out=q_sb[b][:, pair, :], in_=q_rows[:, pair, :])
+                nc.sync.dma_start(
+                    out=kv_sb[b][c][:].rearrange("p (u e) n -> p u (e n)", u=HALVES),
+                    in_=kv_rows[c],
+                )
+            nc.sync.dma_start(out=v_sb[b][:], in_=v[b].rearrange("(i p) n -> p i n", p=P))
+        w_rows = w_proj.rearrange("(g u p e) n -> g p u (e n)", g=PASSES, u=HALVES, p=P, e=2)
+        for g in range(PASSES):
+            nc.sync.dma_start(
+                out=w_sb[g][:].rearrange("p (u e) n -> p u (e n)", u=HALVES), in_=w_rows[g]
+            )
+        nc.sync.dma_start(out=bias_bc[:], in_=b_proj.partition_broadcast(P))
+
+        q2_codes = keep.tile([P, ALL_TILES, PASSES, P], U32, align_bytes=64)
+        q2_scales = keep.tile([P, ALL_TILES, PASSES, P], U8, align_bytes=64)
+        kv_codes = [
+            keep.tile([P, PASSES, FEAT], U32, name="kv_codes%d" % b, align_bytes=64)
+            for b in range(BATCH)
+        ]
+        kv_scales = [
+            keep.tile([P, PASSES, FEAT], U8, name="kv_scales%d" % b, align_bytes=64)
+            for b in range(BATCH)
+        ]
+        h_codes = keep.tile([P, ALL_TILES, PASSES, P], U32, align_bytes=64)
+        h_scales = keep.tile([P, ALL_TILES, PASSES, P], U8, align_bytes=64)
+        w_codes = keep.tile([P, PASSES, OUT_COLS], U32, align_bytes=64)
+        w_scales = keep.tile([P, PASSES, OUT_COLS], U8, align_bytes=64)
+        v_turned = keep.tile([P, ALL_TILES, PASSES, P, SLOTS], BF16)
+
+        sumsq = const.tile([P, ALL_TILES], F32)
+        floored = const.tile([P, ALL_TILES], F32)
+        norm = const.tile([P, ALL_TILES], F32)
+        rnorm = const.tile([P, ALL_TILES], F32)
+        out_rows = out.flatten_outer_dims()
+        live = {}
+
+        def turn_words(rows_bf16, turned_bf16):
+            words = rows_bf16.bitcast(F32)
+            bank = psum.tile([P, PASSES, HALVES, P], F32, tag="bank")
+            for c in range(PASSES):
+                for u in range(HALVES):
+                    first = (c * HALVES + u) * P
+                    nc.tensor.transpose(
+                        out=bank[:, c, u, :], in_=words[:, first : first + P], identity=ident[:]
+                    )
+            nc.scalar.copy(
+                out=turned_bf16.bitcast(F32), in_=bank[:].rearrange("p c u r -> p c r u")
+            )
+
+        def sum_squares(b):
+            for j in range(TILES):
+                i = b * TILES + j
+                squares = scratch.tile([P, FEAT], BF16)
+                nc.scalar.activation(
+                    out=squares[:],
+                    in_=q_sb[b][:, j, :],
+                    func=ACT.Square,
+                    accum_out=sumsq[:, i : i + 1],
+                )
+
+        def scale_queries(b):
+            cols = slice(b * TILES, (b + 1) * TILES)
+            nc.vector.tensor_scalar_max(
+                out=floored[:, cols], in0=sumsq[:, cols], scalar1=EPS_NORM * EPS_NORM
+            )
+            nc.scalar.sqrt(out=norm[:, cols], in_=floored[:, cols])
+            nc.vector.reciprocal(out=rnorm[:, cols], in_=norm[:, cols])
+            q2 = keep.tile([P, TILES, FEAT], BF16, tag="q2")
+            for j in range(TILES):
+                i = b * TILES + j
+                nc.vector.tensor_scalar_mul(
+                    out=q2[:, j, :], in0=q_sb[b][:, j, :], scalar1=rnorm[:, i : i + 1]
+                )
+            live["q2"] = q2
+
+        def turn_queries(b):
+            q2_turned = keep.tile([P, TILES, PASSES, P, SLOTS], BF16, tag="q2_turned", align_bytes=64)
+            for j in range(TILES):
+                turn_words(live["q2"][:, j, :], q2_turned[:, j])
+            live["q2_turned"] = q2_turned
+
+        def quantise_queries(b):
+            for j in range(0, TILES, 2):
+                i = b * TILES + j
+                nc.vector.quantize_mx(
+                    out=q2_codes[:, i : i + 2].rearrange("p i c r -> p (i c r)").bitcast(FP8X4),
+                    scales=q2_scales[:, i : i + 2].rearrange("p i c r -> p (i c r)"),
+                    in_=live["q2_turned"][:, j : j + 2].rearrange("p i c r t -> p (i c r t)"),
+                )
+
+        def turn_values(b):
+            for j in range(TILES):
+                turn_words(v_sb[b][:, j, :], v_turned[:, b * TILES + j])
+
+        def regroup_state(b, c):
+            for g in range(PASSES):
+                grouped = regroup_pool.tile([P, BANK, SLOTS], BF16, tag="grouped", align_bytes=64)
+                for hu in range(HALVES):
+                    first = BANK * g + 256 * hu
+                    src = kv_sb[b][c][:, :, first : first + 256].rearrange(
+                        "p t (m e) -> p e m t", e=2
+                    )
+                    dst = grouped[:, 256 * hu : 256 * hu + 256, :].rearrange(
+                        "p (e m) t -> p e m t", e=2
+                    )
+                    if g * HALVES + hu >= PASSES * HALVES - KV_ON_SCALAR[b]:
+                        nc.scalar.copy(out=dst, in_=src)
+                    else:
+                        nc.vector.tensor_copy(out=dst, in_=src)
+                live["kv", g] = grouped
+
+        def quantise_state(b, c):
+            for g in range(PASSES):
+                cols = slice(BANK * g, BANK * g + BANK)
+                nc.vector.quantize_mx(
+                    out=kv_codes[b][:, c, cols].bitcast(FP8X4),
+                    scales=kv_scales[b][:, c, cols],
+                    in_=live["kv", g][:].rearrange("p n t -> p (n t)"),
+                )
+
+        def regroup_weights(j):
+            for g in range(PASSES):
+                grouped = regroup_pool.tile([P, BANK, SLOTS], BF16, tag="grouped", align_bytes=64)
+                for hu in range(HALVES):
+                    first = BANK * j + 256 * hu
+                    src = w_sb[g][:, :, first : first + 256].rearrange("p t n -> p n t")
+                    dst = grouped[:, 256 * hu : 256 * hu + 256, :]
+                    if hu >= HALVES - W_ON_SCALAR[j]:
+                        nc.scalar.copy(out=dst, in_=src)
+                    else:
+                        nc.vector.tensor_copy(out=dst, in_=src)
+                live["w", g] = grouped
+
+        def quantise_weights(j):
+            cols = slice(BANK * j, BANK * j + BANK)
+            for g in range(PASSES):
+                nc.vector.quantize_mx(
+                    out=w_codes[:, g, cols].bitcast(FP8X4),
+                    scales=w_scales[:, g, cols],
+                    in_=live["w", g][:].rearrange("p n t -> p (n t)"),
+                )
+
+        def quantise_h(i, h_grouped):
+            nc.vector.quantize_mx(
+                out=h_codes[:, i].rearrange("p g r -> p (g r)").bitcast(FP8X4),
+                scales=h_scales[:, i].rearrange("p g r -> p (g r)"),
+                in_=h_grouped[:].rearrange("p g r t -> p (g r t)"),
+            )
+
+        def first_product(b):
+            waiting = None
+            for i in range(b * TILES, (b + 1) * TILES):
+                h_grouped = h_pool.tile([P, PASSES, P, SLOTS], BF16, align_bytes=64)
+                for g in range(PASSES):
+                    t2_bank = psum.tile([P, SLOTS, P], F32, tag="bank")
+                    for t in range(SLOTS):
+                        cols = slice(BANK * g + P * t, BANK * g + P * t + P)
+                        for c in range(PASSES):
+                            nc.tensor.matmul_mx(
+                                out=t2_bank[:, t, :],
+                                lhsT=kv_codes[b][:, c, cols].bitcast(FP8X4),
+                                lhsT_scale=kv_scales[b][:, c, cols],
+                                rhs=q2_codes[:, i, c, :].bitcast(FP8X4),
+                                rhs_scale=q2_scales[:, i, c, :],
+                                start=(c == 0),
+                                stop=(c == PASSES - 1),
+                            )
+                    nc.vector.scalar_tensor_tensor(
+                        out=h_grouped[:, g],
+                        in0=t2_bank[:].rearrange("p t r -> p r t"),
+                        scalar=1.0 / math.sqrt(TOKENS),
+                        in1=v_turned[:, i, g],
+                        op0=ALU.mult,
+                        op1=ALU.add,
+                    )
+                if waiting is not None:
+                    quantise_h(*waiting)
+                waiting = (i, h_grouped)
+            quantise_h(*waiting)
+
+        def second_product(i, j):
+            cols = slice(BANK * j, BANK * j + BANK)
+            out_bank = psum.tile([P, BANK], F32, tag="bank")
+            for g in range(PASSES):
+                nc.tensor.matmul_mx(
+                    out=out_bank[:],
+                    lhsT=h_codes[:, i, g, :].bitcast(FP8X4),
+                    lhsT_scale=h_scales[:, i, g, :],
+                    rhs=w_codes[:, g, cols].bitcast(FP8X4),
+                    rhs_scale=w_scales[:, g, cols],
+                    start=(g == 0),
+                    stop=(g == PASSES - 1),
+                )
+            result = store_pool.tile([P, BANK], F32)
+            nc.vector.tensor_tensor(
+                out=result[:], in0=out_bank[:], in1=bias_bc[:, cols], op=ALU.add
+            )
+            nc.sync.dma_start(out=out_rows[i * P : (i + 1) * P, cols], in_=result[:])
+
+        for b in range(BATCH):
+            sum_squares(b)
+            regroup_state(b, 0)
+            quantise_state(b, 0)
+            scale_queries(b)
+            regroup_state(b, 1)
+            turn_queries(b)
+            quantise_state(b, 1)
+            quantise_queries(b)
+            turn_values(b)
+            first_product(b)
+        for j in range(OUT_COLS // BANK):
+            regroup_weights(j)
+            quantise_weights(j)
+            for i in range(ALL_TILES):
+                second_product(i, j)

@@ -26,8 +26,9 @@ TILES = TOKENS // P
 ALL_TILES = BATCH * TILES
 BANK = 512
 
-KV_ON_SCALAR = (1, 2)
-W_ON_SCALAR = (2, 2)
+PAIR = 2
+PAIRS = TILES // PAIR
+RUN = 4
 
 FLOPS = 2 * BATCH * TOKENS * FEAT * FEAT + 2 * BATCH * TOKENS * FEAT * OUT_COLS
 
@@ -39,10 +40,12 @@ def tile_essattn_pb_kernel(tc, q_feat, kv, v, w_proj, b_proj, out):
         inputs = ctx.enter_context(tc.tile_pool(name="inputs", bufs=1))
         keep = ctx.enter_context(tc.tile_pool(name="keep", bufs=1))
         scratch = ctx.enter_context(tc.tile_pool(name="scratch", bufs=2))
-        regroup_pool = ctx.enter_context(tc.tile_pool(name="regroup", bufs=5))
+        regroup_pool = ctx.enter_context(tc.tile_pool(name="regroup", bufs=6))
         h_pool = ctx.enter_context(tc.tile_pool(name="h", bufs=4))
         store_pool = ctx.enter_context(tc.tile_pool(name="store", bufs=8))
-        psum = ctx.enter_context(tc.psum_pool(name="psum", bufs=8))
+        psum_turn = ctx.enter_context(tc.psum_pool(name="psum_turn", bufs=2))
+        psum_first = ctx.enter_context(tc.psum_pool(name="psum_first", bufs=3))
+        psum_second = ctx.enter_context(tc.psum_pool(name="psum_second", bufs=3))
 
         one = const.tile([P, 1], F32)
         nc.vector.memset(one[:], 1.0)
@@ -60,24 +63,28 @@ def tile_essattn_pb_kernel(tc, q_feat, kv, v, w_proj, b_proj, out):
         w_sb = [inputs.tile([P, SLOTS, OUT_COLS], BF16, name="w_sb%d" % g) for g in range(PASSES)]
         bias_bc = const.tile([P, OUT_COLS], BF16)
 
+        def load_values(b):
+            nc.sync.dma_start(out=v_sb[b][:], in_=v[b].rearrange("(i p) n -> p i n", p=P))
+
         for b in range(BATCH):
             q_rows = q_feat[b].rearrange("(i p) k -> p i k", p=P)
             kv_rows = kv[b].rearrange(
                 "(c u p e) n -> c p u (e n)", c=PASSES, u=HALVES, p=P, e=2
             )
             for c in range(PASSES):
-                pair = slice(2 * c, 2 * c + 2)
+                pair = slice(PAIR * c, PAIR * c + PAIR)
                 nc.sync.dma_start(out=q_sb[b][:, pair, :], in_=q_rows[:, pair, :])
                 nc.sync.dma_start(
                     out=kv_sb[b][c][:].rearrange("p (u e) n -> p u (e n)", u=HALVES),
                     in_=kv_rows[c],
                 )
-            nc.sync.dma_start(out=v_sb[b][:], in_=v[b].rearrange("(i p) n -> p i n", p=P))
+        load_values(0)
         w_rows = w_proj.rearrange("(g u p e) n -> g p u (e n)", g=PASSES, u=HALVES, p=P, e=2)
         for g in range(PASSES):
             nc.sync.dma_start(
                 out=w_sb[g][:].rearrange("p (u e) n -> p u (e n)", u=HALVES), in_=w_rows[g]
             )
+        load_values(1)
         nc.sync.dma_start(out=bias_bc[:], in_=b_proj.partition_broadcast(P))
 
         q2_codes = keep.tile([P, ALL_TILES, PASSES, P], U32, align_bytes=64)
@@ -101,11 +108,10 @@ def tile_essattn_pb_kernel(tc, q_feat, kv, v, w_proj, b_proj, out):
         norm = const.tile([P, ALL_TILES], F32)
         rnorm = const.tile([P, ALL_TILES], F32)
         out_rows = out.flatten_outer_dims()
-        live = {}
 
         def turn_words(rows_bf16, turned_bf16):
             words = rows_bf16.bitcast(F32)
-            bank = psum.tile([P, PASSES, HALVES, P], F32, tag="bank")
+            bank = psum_turn.tile([P, PASSES, HALVES, P], F32, tag="turn")
             for c in range(PASSES):
                 for u in range(HALVES):
                     first = (c * HALVES + u) * P
@@ -116,97 +122,87 @@ def tile_essattn_pb_kernel(tc, q_feat, kv, v, w_proj, b_proj, out):
                 out=turned_bf16.bitcast(F32), in_=bank[:].rearrange("p c u r -> p c r u")
             )
 
-        def sum_squares(b):
-            for j in range(TILES):
-                i = b * TILES + j
-                squares = scratch.tile([P, FEAT], BF16)
-                nc.scalar.activation(
-                    out=squares[:],
-                    in_=q_sb[b][:, j, :],
-                    func=ACT.Square,
-                    accum_out=sumsq[:, i : i + 1],
-                )
-
-        def scale_queries(b):
-            cols = slice(b * TILES, (b + 1) * TILES)
-            nc.vector.tensor_scalar_max(
-                out=floored[:, cols], in0=sumsq[:, cols], scalar1=EPS_NORM * EPS_NORM
-            )
-            nc.scalar.sqrt(out=norm[:, cols], in_=floored[:, cols])
-            nc.vector.reciprocal(out=rnorm[:, cols], in_=norm[:, cols])
-            q2 = keep.tile([P, TILES, FEAT], BF16, tag="q2")
-            for j in range(TILES):
-                i = b * TILES + j
-                nc.vector.tensor_scalar_mul(
-                    out=q2[:, j, :], in0=q_sb[b][:, j, :], scalar1=rnorm[:, i : i + 1]
-                )
-            live["q2"] = q2
-
-        def turn_queries(b):
-            q2_turned = keep.tile([P, TILES, PASSES, P, SLOTS], BF16, tag="q2_turned", align_bytes=64)
-            for j in range(TILES):
-                turn_words(live["q2"][:, j, :], q2_turned[:, j])
-            live["q2_turned"] = q2_turned
-
         def quantise_queries(b):
-            for j in range(0, TILES, 2):
-                i = b * TILES + j
+            for pair in range(PAIRS):
+                first_j = pair * PAIR
+                first_i = b * TILES + first_j
+                cols = slice(first_i, first_i + PAIR)
+                for j in range(first_j, first_j + PAIR):
+                    i = b * TILES + j
+                    squares = scratch.tile([P, FEAT], BF16)
+                    nc.scalar.activation(
+                        out=squares[:],
+                        in_=q_sb[b][:, j, :],
+                        func=ACT.Square,
+                        accum_out=sumsq[:, i : i + 1],
+                    )
+                nc.vector.tensor_scalar_max(
+                    out=floored[:, cols], in0=sumsq[:, cols], scalar1=EPS_NORM * EPS_NORM
+                )
+                nc.scalar.sqrt(out=norm[:, cols], in_=floored[:, cols])
+                nc.vector.reciprocal(out=rnorm[:, cols], in_=norm[:, cols])
+                q2 = scratch.tile([P, PAIR, FEAT], BF16)
+                q2_turned = scratch.tile([P, PAIR, PASSES, P, SLOTS], BF16, align_bytes=64)
+                for k in range(PAIR):
+                    i = first_i + k
+                    nc.vector.tensor_scalar_mul(
+                        out=q2[:, k, :], in0=q_sb[b][:, first_j + k, :], scalar1=rnorm[:, i : i + 1]
+                    )
+                for k in range(PAIR):
+                    turn_words(q2[:, k, :], q2_turned[:, k])
                 nc.vector.quantize_mx(
-                    out=q2_codes[:, i : i + 2].rearrange("p i c r -> p (i c r)").bitcast(FP8X4),
-                    scales=q2_scales[:, i : i + 2].rearrange("p i c r -> p (i c r)"),
-                    in_=live["q2_turned"][:, j : j + 2].rearrange("p i c r t -> p (i c r t)"),
+                    out=q2_codes[:, cols].rearrange("p i c r -> p (i c r)").bitcast(FP8X4),
+                    scales=q2_scales[:, cols].rearrange("p i c r -> p (i c r)"),
+                    in_=q2_turned[:].rearrange("p i c r t -> p (i c r t)"),
                 )
 
         def turn_values(b):
             for j in range(TILES):
                 turn_words(v_sb[b][:, j, :], v_turned[:, b * TILES + j])
 
-        def regroup_state(b, c):
-            for g in range(PASSES):
-                grouped = regroup_pool.tile([P, BANK, SLOTS], BF16, tag="grouped", align_bytes=64)
-                for hu in range(HALVES):
-                    first = BANK * g + 256 * hu
-                    src = kv_sb[b][c][:, :, first : first + 256].rearrange(
-                        "p t (m e) -> p e m t", e=2
-                    )
-                    dst = grouped[:, 256 * hu : 256 * hu + 256, :].rearrange(
-                        "p (e m) t -> p e m t", e=2
-                    )
-                    if g * HALVES + hu >= PASSES * HALVES - KV_ON_SCALAR[b]:
-                        nc.scalar.copy(out=dst, in_=src)
-                    else:
+        def quantise_state(b):
+            for c in range(PASSES):
+                chunks = []
+                for g in range(PASSES):
+                    grouped = regroup_pool.tile([P, BANK, SLOTS], BF16, tag="grouped", align_bytes=64)
+                    for hu in range(HALVES):
+                        first = BANK * g + 256 * hu
+                        src = kv_sb[b][c][:, :, first : first + 256].rearrange(
+                            "p t (m i e) -> p e m t i", i=RUN, e=2
+                        )
+                        dst = grouped[:, 256 * hu : 256 * hu + 256, :].rearrange(
+                            "p (e m i) t -> p e m t i", e=2, i=RUN
+                        )
                         nc.vector.tensor_copy(out=dst, in_=src)
-                live["kv", g] = grouped
+                    chunks.append(grouped)
+                for g in range(PASSES):
+                    cols = slice(BANK * g, BANK * g + BANK)
+                    nc.vector.quantize_mx(
+                        out=kv_codes[b][:, c, cols].bitcast(FP8X4),
+                        scales=kv_scales[b][:, c, cols],
+                        in_=chunks[g][:].rearrange("p n t -> p (n t)"),
+                    )
 
-        def quantise_state(b, c):
-            for g in range(PASSES):
-                cols = slice(BANK * g, BANK * g + BANK)
-                nc.vector.quantize_mx(
-                    out=kv_codes[b][:, c, cols].bitcast(FP8X4),
-                    scales=kv_scales[b][:, c, cols],
-                    in_=live["kv", g][:].rearrange("p n t -> p (n t)"),
-                )
-
-        def regroup_weights(j):
+        def quantise_weights(j):
+            chunks = []
             for g in range(PASSES):
                 grouped = regroup_pool.tile([P, BANK, SLOTS], BF16, tag="grouped", align_bytes=64)
                 for hu in range(HALVES):
                     first = BANK * j + 256 * hu
-                    src = w_sb[g][:, :, first : first + 256].rearrange("p t n -> p n t")
-                    dst = grouped[:, 256 * hu : 256 * hu + 256, :]
-                    if hu >= HALVES - W_ON_SCALAR[j]:
-                        nc.scalar.copy(out=dst, in_=src)
-                    else:
-                        nc.vector.tensor_copy(out=dst, in_=src)
-                live["w", g] = grouped
-
-        def quantise_weights(j):
+                    src = w_sb[g][:, :, first : first + 256].rearrange(
+                        "p t (m i) -> p m t i", i=RUN
+                    )
+                    dst = grouped[:, 256 * hu : 256 * hu + 256, :].rearrange(
+                        "p (m i) t -> p m t i", i=RUN
+                    )
+                    nc.scalar.copy(out=dst, in_=src)
+                chunks.append(grouped)
             cols = slice(BANK * j, BANK * j + BANK)
             for g in range(PASSES):
                 nc.vector.quantize_mx(
                     out=w_codes[:, g, cols].bitcast(FP8X4),
                     scales=w_scales[:, g, cols],
-                    in_=live["w", g][:].rearrange("p n t -> p (n t)"),
+                    in_=chunks[g][:].rearrange("p n t -> p (n t)"),
                 )
 
         def quantise_h(i, h_grouped):
@@ -221,7 +217,7 @@ def tile_essattn_pb_kernel(tc, q_feat, kv, v, w_proj, b_proj, out):
             for i in range(b * TILES, (b + 1) * TILES):
                 h_grouped = h_pool.tile([P, PASSES, P, SLOTS], BF16, align_bytes=64)
                 for g in range(PASSES):
-                    t2_bank = psum.tile([P, SLOTS, P], F32, tag="bank")
+                    t2_bank = psum_first.tile([P, SLOTS, P], F32)
                     for t in range(SLOTS):
                         cols = slice(BANK * g + P * t, BANK * g + P * t + P)
                         for c in range(PASSES):
@@ -249,7 +245,7 @@ def tile_essattn_pb_kernel(tc, q_feat, kv, v, w_proj, b_proj, out):
 
         def second_product(i, j):
             cols = slice(BANK * j, BANK * j + BANK)
-            out_bank = psum.tile([P, BANK], F32, tag="bank")
+            out_bank = psum_second.tile([P, BANK], F32)
             for g in range(PASSES):
                 nc.tensor.matmul_mx(
                     out=out_bank[:],
@@ -266,19 +262,20 @@ def tile_essattn_pb_kernel(tc, q_feat, kv, v, w_proj, b_proj, out):
             )
             nc.sync.dma_start(out=out_rows[i * P : (i + 1) * P, cols], in_=result[:])
 
-        for b in range(BATCH):
-            sum_squares(b)
-            regroup_state(b, 0)
-            quantise_state(b, 0)
-            scale_queries(b)
-            regroup_state(b, 1)
-            turn_queries(b)
-            quantise_state(b, 1)
-            quantise_queries(b)
-            turn_values(b)
-            first_product(b)
-        for j in range(OUT_COLS // BANK):
-            regroup_weights(j)
+        column_halves = range(OUT_COLS // BANK)
+        quantise_queries(0)
+        quantise_state(0)
+        turn_values(0)
+        first_product(0)
+        quantise_queries(1)
+        quantise_state(1)
+        turn_values(1)
+        for j in column_halves:
             quantise_weights(j)
-            for i in range(ALL_TILES):
+        for j in column_halves:
+            for i in range(TILES):
+                second_product(i, j)
+        first_product(1)
+        for i in range(TILES, ALL_TILES):
+            for j in column_halves:
                 second_product(i, j)

@@ -173,7 +173,11 @@ def tile_essattn_pb_kernel(tc, q_feat, kv, v, w_proj, b_proj, out):
                         dst = grouped[:, 256 * hu : 256 * hu + 256, :].rearrange(
                             "p (e m i) t -> p e m t i", e=2, i=RUN
                         )
-                        nc.vector.tensor_copy(out=dst, in_=src)
+                        if b == 1 and g == PASSES - 1 and hu == HALVES - 1:
+                            for e in range(2):
+                                nc.scalar.copy(out=dst[:, e], in_=src[:, e])
+                        else:
+                            nc.vector.tensor_copy(out=dst, in_=src)
                     chunks.append(grouped)
                 for g in range(PASSES):
                     cols = slice(BANK * g, BANK * g + BANK)
@@ -257,9 +261,15 @@ def tile_essattn_pb_kernel(tc, q_feat, kv, v, w_proj, b_proj, out):
                     stop=(g == PASSES - 1),
                 )
             result = store_pool.tile([P, BANK], F32)
-            nc.vector.tensor_tensor(
-                out=result[:], in0=out_bank[:], in1=bias_bc[:, cols], op=ALU.add
-            )
+            if i < TILES and j == 1:
+                nc.scalar.copy(out=result[:], in_=out_bank[:])
+                nc.gpsimd.tensor_tensor(
+                    out=result[:], in0=result[:], in1=bias_bc[:, cols], op=ALU.add
+                )
+            else:
+                nc.vector.tensor_tensor(
+                    out=result[:], in0=out_bank[:], in1=bias_bc[:, cols], op=ALU.add
+                )
             nc.sync.dma_start(out=out_rows[i * P : (i + 1) * P, cols], in_=result[:])
 
         column_halves = range(OUT_COLS // BANK)

@@ -40,19 +40,24 @@ def tile_essattn_pb_kernel(tc, q_feat, kv, v, w_proj, b_proj, out):
         inputs = ctx.enter_context(tc.tile_pool(name="inputs", bufs=1))
         keep = ctx.enter_context(tc.tile_pool(name="keep", bufs=1))
         scratch = ctx.enter_context(tc.tile_pool(name="scratch", bufs=2))
-        regroup_pool = ctx.enter_context(tc.tile_pool(name="regroup", bufs=6))
+        regroup_pool = ctx.enter_context(tc.tile_pool(name="regroup", bufs=9))
         h_pool = ctx.enter_context(tc.tile_pool(name="h", bufs=4))
         store_pool = ctx.enter_context(tc.tile_pool(name="store", bufs=8))
-        psum_turn = ctx.enter_context(tc.psum_pool(name="psum_turn", bufs=2))
-        psum_first = ctx.enter_context(tc.psum_pool(name="psum_first", bufs=3))
-        psum_second = ctx.enter_context(tc.psum_pool(name="psum_second", bufs=3))
+        psum = ctx.enter_context(tc.psum_pool(name="psum", bufs=8))
+        ctx.enter_context(tc.manual_schedule())
 
         one = const.tile([P, 1], F32)
         nc.vector.memset(one[:], 1.0)
         table_warm = const.tile([P, 1], F32)
         nc.scalar.sqrt(out=table_warm[:], in_=one[:])
+        bias_row = const.tile([P, OUT_COLS], BF16)
+        nc.vector.memset(bias_row[:], 0.0)
+        ones = const.tile([P, P], BF16)
+        nc.vector.memset(ones[:], 1.0)
         ident = const.tile([P, P], F32)
         make_identity(nc, ident[:])
+        ident_bf = const.tile([P, P], BF16)
+        nc.vector.tensor_copy(out=ident_bf[:], in_=ident[:])
 
         q_sb = [inputs.tile([P, TILES, FEAT], BF16, name="q_sb%d" % b) for b in range(BATCH)]
         v_sb = [inputs.tile([P, TILES, FEAT], BF16, name="v_sb%d" % b) for b in range(BATCH)]
@@ -61,12 +66,9 @@ def tile_essattn_pb_kernel(tc, q_feat, kv, v, w_proj, b_proj, out):
             for b in range(BATCH)
         ]
         w_sb = [inputs.tile([P, SLOTS, OUT_COLS], BF16, name="w_sb%d" % g) for g in range(PASSES)]
-        bias_bc = const.tile([P, OUT_COLS], BF16)
+        bias_bc = const.tile([P, OUT_COLS], F32)
 
-        def load_values(b):
-            nc.sync.dma_start(out=v_sb[b][:], in_=v[b].rearrange("(i p) n -> p i n", p=P))
-
-        for b in range(BATCH):
+        def load_queries_and_state(b):
             q_rows = q_feat[b].rearrange("(i p) k -> p i k", p=P)
             kv_rows = kv[b].rearrange(
                 "(c u p e) n -> c p u (e n)", c=PASSES, u=HALVES, p=P, e=2
@@ -78,14 +80,20 @@ def tile_essattn_pb_kernel(tc, q_feat, kv, v, w_proj, b_proj, out):
                     out=kv_sb[b][c][:].rearrange("p (u e) n -> p u (e n)", u=HALVES),
                     in_=kv_rows[c],
                 )
+
+        def load_values(b):
+            nc.sync.dma_start(out=v_sb[b][:], in_=v[b].rearrange("(i p) n -> p i n", p=P))
+
+        nc.scalar.dma_start(out=bias_row[0:1, :], in_=b_proj.unsqueeze(0))
+        load_queries_and_state(0)
         load_values(0)
         w_rows = w_proj.rearrange("(g u p e) n -> g p u (e n)", g=PASSES, u=HALVES, p=P, e=2)
         for g in range(PASSES):
             nc.sync.dma_start(
                 out=w_sb[g][:].rearrange("p (u e) n -> p u (e n)", u=HALVES), in_=w_rows[g]
             )
+        load_queries_and_state(1)
         load_values(1)
-        nc.sync.dma_start(out=bias_bc[:], in_=b_proj.partition_broadcast(P))
 
         q2_codes = keep.tile([P, ALL_TILES, PASSES, P], U32, align_bytes=64)
         q2_scales = keep.tile([P, ALL_TILES, PASSES, P], U8, align_bytes=64)
@@ -109,9 +117,18 @@ def tile_essattn_pb_kernel(tc, q_feat, kv, v, w_proj, b_proj, out):
         rnorm = const.tile([P, ALL_TILES], F32)
         out_rows = out.flatten_outer_dims()
 
+        def spread_bias():
+            for j in range(OUT_COLS // BANK):
+                cols = slice(BANK * j, BANK * j + BANK)
+                bank = psum.tile([P, BANK], F32, tag="bank")
+                nc.tensor.matmul(
+                    out=bank[:], lhsT=ones[:], rhs=bias_row[:, cols], start=True, stop=True
+                )
+                nc.scalar.copy(out=bias_bc[:, cols], in_=bank[:])
+
         def turn_words(rows_bf16, turned_bf16):
             words = rows_bf16.bitcast(F32)
-            bank = psum_turn.tile([P, PASSES, HALVES, P], F32, tag="turn")
+            bank = psum.tile([P, PASSES, HALVES, P], F32, tag="bank")
             for c in range(PASSES):
                 for u in range(HALVES):
                     first = (c * HALVES + u) * P
@@ -122,92 +139,130 @@ def tile_essattn_pb_kernel(tc, q_feat, kv, v, w_proj, b_proj, out):
                 out=turned_bf16.bitcast(F32), in_=bank[:].rearrange("p c u r -> p c r u")
             )
 
-        def quantise_queries(b):
-            for pair in range(PAIRS):
-                first_j = pair * PAIR
-                first_i = b * TILES + first_j
-                cols = slice(first_i, first_i + PAIR)
-                for j in range(first_j, first_j + PAIR):
-                    i = b * TILES + j
-                    squares = scratch.tile([P, FEAT], BF16)
-                    nc.scalar.activation(
-                        out=squares[:],
-                        in_=q_sb[b][:, j, :],
-                        func=ACT.Square,
-                        accum_out=sumsq[:, i : i + 1],
-                    )
-                nc.vector.tensor_scalar_max(
-                    out=floored[:, cols], in0=sumsq[:, cols], scalar1=EPS_NORM * EPS_NORM
+        def square(b, j, on_vector=False):
+            i = b * TILES + j
+            squares = scratch.tile([P, FEAT], BF16, tag="squares")
+            if on_vector:
+                nc.vector.scalar_tensor_tensor(
+                    out=squares[:],
+                    in0=q_sb[b][:, j, :],
+                    scalar=1.0,
+                    in1=q_sb[b][:, j, :],
+                    op0=ALU.mult,
+                    op1=ALU.mult,
+                    accum_out=sumsq[:, i : i + 1],
                 )
-                nc.scalar.sqrt(out=norm[:, cols], in_=floored[:, cols])
-                nc.vector.reciprocal(out=rnorm[:, cols], in_=norm[:, cols])
-                q2 = scratch.tile([P, PAIR, FEAT], BF16)
-                q2_turned = scratch.tile([P, PAIR, PASSES, P, SLOTS], BF16, align_bytes=64)
-                for k in range(PAIR):
-                    i = first_i + k
-                    nc.vector.tensor_scalar_mul(
-                        out=q2[:, k, :], in0=q_sb[b][:, first_j + k, :], scalar1=rnorm[:, i : i + 1]
-                    )
-                for k in range(PAIR):
-                    turn_words(q2[:, k, :], q2_turned[:, k])
-                nc.vector.quantize_mx(
-                    out=q2_codes[:, cols].rearrange("p i c r -> p (i c r)").bitcast(FP8X4),
-                    scales=q2_scales[:, cols].rearrange("p i c r -> p (i c r)"),
-                    in_=q2_turned[:].rearrange("p i c r t -> p (i c r t)"),
+                return
+            nc.scalar.activation(
+                out=squares[:],
+                in_=q_sb[b][:, j, :],
+                func=ACT.Square,
+                accum_out=sumsq[:, i : i + 1],
+            )
+
+        def pair_cols(b, pair):
+            first_i = b * TILES + pair * PAIR
+            return slice(first_i, first_i + PAIR)
+
+        def root(b, pair):
+            cols = pair_cols(b, pair)
+            nc.scalar.sqrt(out=norm[:, cols], in_=sumsq[:, cols])
+
+        def invert(b, pair):
+            cols = pair_cols(b, pair)
+            nc.vector.tensor_scalar_max(out=floored[:, cols], in0=norm[:, cols], scalar1=EPS_NORM)
+            nc.vector.reciprocal(out=rnorm[:, cols], in_=floored[:, cols])
+
+        def scale_queries(b, pair):
+            q2 = scratch.tile([P, PAIR, FEAT], BF16, tag="q2")
+            for k in range(PAIR):
+                i = b * TILES + pair * PAIR + k
+                nc.vector.tensor_scalar_mul(
+                    out=q2[:, k, :], in0=q_sb[b][:, pair * PAIR + k, :], scalar1=rnorm[:, i : i + 1]
                 )
+            return q2
 
-        def turn_values(b):
-            for j in range(TILES):
-                turn_words(v_sb[b][:, j, :], v_turned[:, b * TILES + j])
+        def turn_queries(q2):
+            q2_turned = scratch.tile([P, PAIR, PASSES, P, SLOTS], BF16, tag="turned", align_bytes=64)
+            for k in range(PAIR):
+                turn_words(q2[:, k, :], q2_turned[:, k])
+            return q2_turned
 
-        def quantise_state(b):
-            for c in range(PASSES):
-                chunks = []
-                for g in range(PASSES):
-                    grouped = regroup_pool.tile([P, BANK, SLOTS], BF16, tag="grouped", align_bytes=64)
-                    for hu in range(HALVES):
-                        first = BANK * g + 256 * hu
-                        src = kv_sb[b][c][:, :, first : first + 256].rearrange(
-                            "p t (m i e) -> p e m t i", i=RUN, e=2
-                        )
-                        dst = grouped[:, 256 * hu : 256 * hu + 256, :].rearrange(
-                            "p (e m i) t -> p e m t i", e=2, i=RUN
-                        )
-                        if b == 1 and g == PASSES - 1 and hu == HALVES - 1:
-                            for e in range(2):
-                                nc.scalar.copy(out=dst[:, e], in_=src[:, e])
-                        else:
-                            nc.vector.tensor_copy(out=dst, in_=src)
-                    chunks.append(grouped)
-                for g in range(PASSES):
-                    cols = slice(BANK * g, BANK * g + BANK)
-                    nc.vector.quantize_mx(
-                        out=kv_codes[b][:, c, cols].bitcast(FP8X4),
-                        scales=kv_scales[b][:, c, cols],
-                        in_=chunks[g][:].rearrange("p n t -> p (n t)"),
-                    )
+        def quantise_queries(b, pair, q2_turned):
+            cols = pair_cols(b, pair)
+            nc.vector.quantize_mx(
+                out=q2_codes[:, cols].rearrange("p i c r -> p (i c r)").bitcast(FP8X4),
+                scales=q2_scales[:, cols].rearrange("p i c r -> p (i c r)"),
+                in_=q2_turned[:].rearrange("p i c r t -> p (i c r t)"),
+            )
 
-        def quantise_weights(j):
-            chunks = []
-            for g in range(PASSES):
-                grouped = regroup_pool.tile([P, BANK, SLOTS], BF16, tag="grouped", align_bytes=64)
-                for hu in range(HALVES):
-                    first = BANK * j + 256 * hu
-                    src = w_sb[g][:, :, first : first + 256].rearrange(
-                        "p t (m i) -> p m t i", i=RUN
-                    )
-                    dst = grouped[:, 256 * hu : 256 * hu + 256, :].rearrange(
-                        "p (m i) t -> p m t i", i=RUN
-                    )
-                    nc.scalar.copy(out=dst, in_=src)
-                chunks.append(grouped)
+        def turn_values(b, j):
+            turn_words(v_sb[b][:, j, :], v_turned[:, b * TILES + j])
+
+        def on_tensor(dst, src):
+            bank = psum.tile([P, BANK], F32, tag="bank")
+            values = bank[:].bitcast(BF16)
+            for half in range(2):
+                nc.tensor.matmul(
+                    out=values[:, BANK * half : BANK * half + BANK],
+                    lhsT=ident_bf[:],
+                    rhs=src[half],
+                    start=True,
+                    stop=True,
+                )
+            nc.scalar.copy(out=dst.rearrange("p n t -> p (n t)").bitcast(F32), in_=bank[:])
+
+        def new_group():
+            grouped = regroup_pool.tile([P, BANK, SLOTS], BF16, tag="grouped", align_bytes=64)
+            return grouped
+
+        def regroup_state(grouped, b, c, g, hu, engine):
+            first = BANK * g + 256 * hu
+            rows = kv_sb[b][c][:, :, first : first + 256]
+            here = grouped[:, 256 * hu : 256 * hu + 256, :]
+            if engine == "tensor":
+                on_tensor(here, [rows[:, :, e::2].rearrange("p t m -> p m t") for e in range(2)])
+                return
+            src = rows.rearrange("p t (m i e) -> p e m t i", i=RUN, e=2)
+            dst = here.rearrange("p (e m i) t -> p e m t i", e=2, i=RUN)
+            if engine == "scalar":
+                for e in range(2):
+                    nc.scalar.copy(out=dst[:, e], in_=src[:, e])
+            else:
+                nc.vector.tensor_copy(out=dst, in_=src)
+
+        def quantise_state(grouped, b, c, g):
+            cols = slice(BANK * g, BANK * g + BANK)
+            nc.vector.quantize_mx(
+                out=kv_codes[b][:, c, cols].bitcast(FP8X4),
+                scales=kv_scales[b][:, c, cols],
+                in_=grouped[:].rearrange("p n t -> p (n t)"),
+            )
+
+        def regroup_weights(grouped, g, j, hu, engine):
+            first = BANK * j + 256 * hu
+            rows = w_sb[g][:, :, first : first + 256]
+            here = grouped[:, 256 * hu : 256 * hu + 256, :]
+            if engine == "tensor":
+                on_tensor(
+                    here,
+                    [rows[:, :, P * e : P * e + P].rearrange("p t m -> p m t") for e in range(2)],
+                )
+                return
+            src = rows.rearrange("p t (m i) -> p m t i", i=RUN)
+            dst = here.rearrange("p (m i) t -> p m t i", i=RUN)
+            if engine == "scalar":
+                nc.scalar.copy(out=dst, in_=src)
+            else:
+                nc.vector.tensor_copy(out=dst, in_=src)
+
+        def quantise_weights(grouped, g, j):
             cols = slice(BANK * j, BANK * j + BANK)
-            for g in range(PASSES):
-                nc.vector.quantize_mx(
-                    out=w_codes[:, g, cols].bitcast(FP8X4),
-                    scales=w_scales[:, g, cols],
-                    in_=chunks[g][:].rearrange("p n t -> p (n t)"),
-                )
+            nc.vector.quantize_mx(
+                out=w_codes[:, g, cols].bitcast(FP8X4),
+                scales=w_scales[:, g, cols],
+                in_=grouped[:].rearrange("p n t -> p (n t)"),
+            )
 
         def quantise_h(i, h_grouped):
             nc.vector.quantize_mx(
@@ -216,40 +271,36 @@ def tile_essattn_pb_kernel(tc, q_feat, kv, v, w_proj, b_proj, out):
                 in_=h_grouped[:].rearrange("p g r t -> p (g r t)"),
             )
 
-        def first_product(b):
-            waiting = None
-            for i in range(b * TILES, (b + 1) * TILES):
-                h_grouped = h_pool.tile([P, PASSES, P, SLOTS], BF16, align_bytes=64)
-                for g in range(PASSES):
-                    t2_bank = psum_first.tile([P, SLOTS, P], F32)
-                    for t in range(SLOTS):
-                        cols = slice(BANK * g + P * t, BANK * g + P * t + P)
-                        for c in range(PASSES):
-                            nc.tensor.matmul_mx(
-                                out=t2_bank[:, t, :],
-                                lhsT=kv_codes[b][:, c, cols].bitcast(FP8X4),
-                                lhsT_scale=kv_scales[b][:, c, cols],
-                                rhs=q2_codes[:, i, c, :].bitcast(FP8X4),
-                                rhs_scale=q2_scales[:, i, c, :],
-                                start=(c == 0),
-                                stop=(c == PASSES - 1),
-                            )
-                    nc.vector.scalar_tensor_tensor(
-                        out=h_grouped[:, g],
-                        in0=t2_bank[:].rearrange("p t r -> p r t"),
-                        scalar=1.0 / math.sqrt(TOKENS),
-                        in1=v_turned[:, i, g],
-                        op0=ALU.mult,
-                        op1=ALU.add,
-                    )
-                if waiting is not None:
-                    quantise_h(*waiting)
-                waiting = (i, h_grouped)
-            quantise_h(*waiting)
+        def first_product(i):
+            b = i // TILES
+            h_grouped = h_pool.tile([P, PASSES, P, SLOTS], BF16, align_bytes=64)
+            for g in range(PASSES):
+                t2_bank = psum.tile([P, SLOTS, P], F32, tag="bank")
+                for t in range(SLOTS):
+                    cols = slice(BANK * g + P * t, BANK * g + P * t + P)
+                    for c in range(PASSES):
+                        nc.tensor.matmul_mx(
+                            out=t2_bank[:, t, :],
+                            lhsT=kv_codes[b][:, c, cols].bitcast(FP8X4),
+                            lhsT_scale=kv_scales[b][:, c, cols],
+                            rhs=q2_codes[:, i, c, :].bitcast(FP8X4),
+                            rhs_scale=q2_scales[:, i, c, :],
+                            start=(c == 0),
+                            stop=(c == PASSES - 1),
+                        )
+                nc.vector.scalar_tensor_tensor(
+                    out=h_grouped[:, g],
+                    in0=t2_bank[:].rearrange("p t r -> p r t"),
+                    scalar=1.0 / math.sqrt(TOKENS),
+                    in1=v_turned[:, i, g],
+                    op0=ALU.mult,
+                    op1=ALU.add,
+                )
+            return h_grouped
 
-        def second_product(i, j):
+        def second_product(i, j, on_vector):
             cols = slice(BANK * j, BANK * j + BANK)
-            out_bank = psum_second.tile([P, BANK], F32)
+            out_bank = psum.tile([P, BANK], F32, tag="bank")
             for g in range(PASSES):
                 nc.tensor.matmul_mx(
                     out=out_bank[:],
@@ -261,31 +312,114 @@ def tile_essattn_pb_kernel(tc, q_feat, kv, v, w_proj, b_proj, out):
                     stop=(g == PASSES - 1),
                 )
             result = store_pool.tile([P, BANK], F32)
-            if i < TILES and j == 1:
+            if on_vector:
+                nc.vector.tensor_tensor(
+                    out=result[:], in0=out_bank[:], in1=bias_bc[:, cols], op=ALU.add
+                )
+            else:
                 nc.scalar.copy(out=result[:], in_=out_bank[:])
                 nc.gpsimd.tensor_tensor(
                     out=result[:], in0=result[:], in1=bias_bc[:, cols], op=ALU.add
                 )
-            else:
-                nc.vector.tensor_tensor(
-                    out=result[:], in0=out_bank[:], in1=bias_bc[:, cols], op=ALU.add
-                )
             nc.sync.dma_start(out=out_rows[i * P : (i + 1) * P, cols], in_=result[:])
 
-        column_halves = range(OUT_COLS // BANK)
-        quantise_queries(0)
-        quantise_state(0)
-        turn_values(0)
-        first_product(0)
-        quantise_queries(1)
-        quantise_state(1)
-        turn_values(1)
-        for j in column_halves:
-            quantise_weights(j)
-        for j in column_halves:
-            for i in range(TILES):
-                second_product(i, j)
-        first_product(1)
+        square(0, 0)
+        square(0, 1, True)
+        root(0, 0)
+        spread_bias()
+        invert(0, 0)
+        q2 = scale_queries(0, 0)
+        turned = turn_queries(q2)
+        groups = [new_group() for g in range(PASSES)]
+        for g in range(PASSES):
+            for hu in range(HALVES):
+                regroup_state(groups[g], 0, 0, g, hu, "vector")
+        square(0, 2)
+        square(0, 3)
+        root(0, 1)
+        quantise_queries(0, 0, turned)
+        quantise_state(groups[0], 0, 0, 0)
+        quantise_state(groups[1], 0, 0, 1)
+        invert(0, 1)
+        groups = [new_group() for g in range(PASSES)]
+        regroup_state(groups[0], 0, 1, 0, 0, "vector")
+        q2 = scale_queries(0, 1)
+        regroup_state(groups[1], 0, 1, 1, 0, "vector")
+        for g in range(PASSES):
+            regroup_state(groups[g], 0, 1, g, 1, "tensor")
+        turned = turn_queries(q2)
+        for g in range(PASSES):
+            quantise_state(groups[g], 0, 1, g)
+        quantise_queries(0, 1, turned)
+        for j in range(TILES):
+            turn_values(0, j)
+        wg = {(g, j): new_group() for g in range(2) for j in range(2)}
+        groups = [[new_group() for g in range(PASSES)] for c in range(PASSES)]
+        h = {}
+        h[0] = first_product(0)
+        for hu in range(HALVES):
+            regroup_weights(wg[0, 0], 0, 0, hu, "vector")
+        h[1] = first_product(1)
+        quantise_h(0, h[0])
+        square(1, 0)
+        square(1, 1)
+        root(1, 0)
+        for hu in range(HALVES):
+            regroup_weights(wg[1, 0], 1, 0, hu, "tensor")
+        h[2] = first_product(2)
+        quantise_h(1, h[1])
+        invert(1, 0)
+        q2a = scale_queries(1, 0)
+        h[3] = first_product(3)
+        turned = turn_queries(q2a)
+        square(1, 2)
+        quantise_h(2, h[2])
+        for hu in range(HALVES):
+            regroup_weights(wg[0, 1], 0, 1, hu, "tensor")
+        regroup_state(groups[0][0], 1, 0, 0, 0, "vector")
+        quantise_weights(wg[0, 0], 0, 0)
+        quantise_h(3, h[3])
+        quantise_weights(wg[1, 0], 1, 0)
+        for hu in range(HALVES):
+            regroup_weights(wg[1, 1], 1, 1, hu, "tensor")
+        square(1, 3)
+        root(1, 1)
+        regroup_state(groups[0][1], 1, 0, 1, 0, "vector")
+        quantise_queries(1, 0, turned)
+        for g in range(PASSES):
+            quantise_weights(wg[g, 1], g, 1)
+        for i in range(TILES):
+            second_product(i, 0, i >= 2)
+        for g in range(2):
+            regroup_state(groups[0][g], 1, 0, g, 1, "tensor")
+        invert(1, 1)
+        q2 = scale_queries(1, 1)
+        for i in range(2):
+            second_product(i, 1, False)
+        turned = turn_queries(q2)
+        quantise_state(groups[0][0], 1, 0, 0)
+        quantise_state(groups[0][1], 1, 0, 1)
+        regroup_state(groups[1][0], 1, 1, 0, 0, "vector")
+        regroup_state(groups[1][1], 1, 1, 1, 0, "vector")
+        regroup_state(groups[1][0], 1, 1, 0, 1, "tensor")
+        regroup_state(groups[1][1], 1, 1, 1, 1, "scalar")
+        quantise_queries(1, 1, turned)
+        for g in range(2):
+            quantise_state(groups[1][g], 1, 1, g)
+        for j in range(TILES):
+            turn_values(1, j)
+        for i in range(2, TILES):
+            second_product(i, 1, False)
+        waiting = None
         for i in range(TILES, ALL_TILES):
-            for j in column_halves:
-                second_product(i, j)
+            h = first_product(i)
+            if waiting is not None:
+                quantise_h(*waiting)
+                if i > TILES + 1:
+                    for j in range(2):
+                        second_product(i - 2, j, j == 0)
+            waiting = (i, h)
+        quantise_h(*waiting)
+        for i in range(ALL_TILES - 2, ALL_TILES):
+            for j in range(2):
+                second_product(i, j, True)

@@ -84,8 +84,8 @@ def tile_essattn_pb_kernel(tc, q_feat, kv, v, w_proj, b_proj, out):
         def load_values(b):
             nc.sync.dma_start(out=v_sb[b][:], in_=v[b].rearrange("(i p) n -> p i n", p=P))
 
-        nc.scalar.dma_start(out=bias_row[0:1, :], in_=b_proj.unsqueeze(0))
         load_queries_and_state(0)
+        nc.sync.dma_start(out=bias_row[0:1, :], in_=b_proj.unsqueeze(0))
         load_values(0)
         w_rows = w_proj.rearrange("(g u p e) n -> g p u (e n)", g=PASSES, u=HALVES, p=P, e=2)
         for g in range(PASSES):
@@ -326,7 +326,6 @@ def tile_essattn_pb_kernel(tc, q_feat, kv, v, w_proj, b_proj, out):
         square(0, 0)
         square(0, 1, True)
         root(0, 0)
-        spread_bias()
         invert(0, 0)
         q2 = scale_queries(0, 0)
         turned = turn_queries(q2)
@@ -353,6 +352,7 @@ def tile_essattn_pb_kernel(tc, q_feat, kv, v, w_proj, b_proj, out):
         quantise_queries(0, 1, turned)
         for j in range(TILES):
             turn_values(0, j)
+        spread_bias()
         wg = {(g, j): new_group() for g in range(2) for j in range(2)}
         groups = [[new_group() for g in range(PASSES)] for c in range(PASSES)]
         h = {}

@@ -343,16 +343,15 @@ def tile_essattn_pb_kernel(tc, q_feat, kv, v, w_proj, b_proj, out):
         groups = [new_group() for g in range(PASSES)]
         regroup_state(groups[0], 0, 1, 0, 0, "vector")
         q2 = scale_queries(0, 1)
-        regroup_state(groups[1], 0, 1, 1, 0, "vector")
-        for g in range(PASSES):
-            regroup_state(groups[g], 0, 1, g, 1, "tensor")
+        regroup_state(groups[0], 0, 1, 0, 1, "tensor")
+        regroup_state(groups[1], 0, 1, 1, 1, "tensor")
+        regroup_state(groups[1], 0, 1, 1, 0, "scalar")
         turned = turn_queries(q2)
         for g in range(PASSES):
             quantise_state(groups[g], 0, 1, g)
         quantise_queries(0, 1, turned)
         for j in range(TILES):
             turn_values(0, j)
-        spread_bias()
         wg = {(g, j): new_group() for g in range(2) for j in range(2)}
         groups = [[new_group() for g in range(PASSES)] for c in range(PASSES)]
         h = {}
@@ -364,6 +363,7 @@ def tile_essattn_pb_kernel(tc, q_feat, kv, v, w_proj, b_proj, out):
         square(1, 0)
         square(1, 1)
         root(1, 0)
+        spread_bias()
         for hu in range(HALVES):
             regroup_weights(wg[1, 0], 1, 0, hu, "tensor")
         h[2] = first_product(2)
@@ -384,32 +384,30 @@ def tile_essattn_pb_kernel(tc, q_feat, kv, v, w_proj, b_proj, out):
             regroup_weights(wg[1, 1], 1, 1, hu, "tensor")
         square(1, 3)
         root(1, 1)
-        regroup_state(groups[0][1], 1, 0, 1, 0, "vector")
         quantise_queries(1, 0, turned)
-        for g in range(PASSES):
-            quantise_weights(wg[g, 1], g, 1)
         for i in range(TILES):
-            second_product(i, 0, i >= 2)
+            second_product(i, 0, True)
         for g in range(2):
             regroup_state(groups[0][g], 1, 0, g, 1, "tensor")
+        regroup_state(groups[0][1], 1, 0, 1, 0, "scalar")
         invert(1, 1)
         q2 = scale_queries(1, 1)
-        for i in range(2):
-            second_product(i, 1, False)
         turned = turn_queries(q2)
+        regroup_state(groups[1][0], 1, 1, 0, 0, "vector")
+        regroup_state(groups[1][0], 1, 1, 0, 1, "tensor")
+        for g in range(PASSES):
+            quantise_weights(wg[g, 1], g, 1)
         quantise_state(groups[0][0], 1, 0, 0)
         quantise_state(groups[0][1], 1, 0, 1)
-        regroup_state(groups[1][0], 1, 1, 0, 0, "vector")
-        regroup_state(groups[1][1], 1, 1, 1, 0, "vector")
-        regroup_state(groups[1][0], 1, 1, 0, 1, "tensor")
-        regroup_state(groups[1][1], 1, 1, 1, 1, "scalar")
+        for hu in range(HALVES):
+            regroup_state(groups[1][1], 1, 1, 1, hu, "scalar")
+        for i in range(TILES):
+            second_product(i, 1, True)
         quantise_queries(1, 1, turned)
-        for g in range(2):
-            quantise_state(groups[1][g], 1, 1, g)
         for j in range(TILES):
             turn_values(1, j)
-        for i in range(2, TILES):
-            second_product(i, 1, False)
+        for g in range(2):
+            quantise_state(groups[1][g], 1, 1, g)
         waiting = None
         for i in range(TILES, ALL_TILES):
             h = first_product(i)
@@ -417,7 +415,7 @@ def tile_essattn_pb_kernel(tc, q_feat, kv, v, w_proj, b_proj, out):
                 quantise_h(*waiting)
                 if i > TILES + 1:
                     for j in range(2):
-                        second_product(i - 2, j, j == 0)
+                        second_product(i - 2, j, True)
             waiting = (i, h)
         quantise_h(*waiting)
         for i in range(ALL_TILES - 2, ALL_TILES):

@@ -41,19 +41,14 @@ def tile_essattn_pb_kernel(tc, q_feat, kv, v, w_proj, b_proj, out):
         keep = ctx.enter_context(tc.tile_pool(name="keep", bufs=1))
         scratch = ctx.enter_context(tc.tile_pool(name="scratch", bufs=2))
         regroup_pool = ctx.enter_context(tc.tile_pool(name="regroup", bufs=9))
-        h_pool = ctx.enter_context(tc.tile_pool(name="h", bufs=4))
+        h_pool = ctx.enter_context(tc.tile_pool(name="h", bufs=6))
         store_pool = ctx.enter_context(tc.tile_pool(name="store", bufs=8))
         psum = ctx.enter_context(tc.psum_pool(name="psum", bufs=8))
-        ctx.enter_context(tc.manual_schedule())
 
         one = const.tile([P, 1], F32)
         nc.vector.memset(one[:], 1.0)
         table_warm = const.tile([P, 1], F32)
         nc.scalar.sqrt(out=table_warm[:], in_=one[:])
-        bias_row = const.tile([P, OUT_COLS], BF16)
-        nc.vector.memset(bias_row[:], 0.0)
-        ones = const.tile([P, P], BF16)
-        nc.vector.memset(ones[:], 1.0)
         ident = const.tile([P, P], F32)
         make_identity(nc, ident[:])
         ident_bf = const.tile([P, P], BF16)
@@ -66,7 +61,7 @@ def tile_essattn_pb_kernel(tc, q_feat, kv, v, w_proj, b_proj, out):
             for b in range(BATCH)
         ]
         w_sb = [inputs.tile([P, SLOTS, OUT_COLS], BF16, name="w_sb%d" % g) for g in range(PASSES)]
-        bias_bc = const.tile([P, OUT_COLS], F32)
+        bias_bc = const.tile([P, OUT_COLS], BF16)
 
         def load_queries_and_state(b):
             q_rows = q_feat[b].rearrange("(i p) k -> p i k", p=P)
@@ -85,7 +80,6 @@ def tile_essattn_pb_kernel(tc, q_feat, kv, v, w_proj, b_proj, out):
             nc.sync.dma_start(out=v_sb[b][:], in_=v[b].rearrange("(i p) n -> p i n", p=P))
 
         load_queries_and_state(0)
-        nc.sync.dma_start(out=bias_row[0:1, :], in_=b_proj.unsqueeze(0))
         load_values(0)
         w_rows = w_proj.rearrange("(g u p e) n -> g p u (e n)", g=PASSES, u=HALVES, p=P, e=2)
         for g in range(PASSES):
@@ -94,6 +88,7 @@ def tile_essattn_pb_kernel(tc, q_feat, kv, v, w_proj, b_proj, out):
             )
         load_queries_and_state(1)
         load_values(1)
+        nc.sync.dma_start(out=bias_bc[:], in_=b_proj.partition_broadcast(P))
 
         q2_codes = keep.tile([P, ALL_TILES, PASSES, P], U32, align_bytes=64)
         q2_scales = keep.tile([P, ALL_TILES, PASSES, P], U8, align_bytes=64)
@@ -116,15 +111,6 @@ def tile_essattn_pb_kernel(tc, q_feat, kv, v, w_proj, b_proj, out):
         norm = const.tile([P, ALL_TILES], F32)
         rnorm = const.tile([P, ALL_TILES], F32)
         out_rows = out.flatten_outer_dims()
-
-        def spread_bias():
-            for j in range(OUT_COLS // BANK):
-                cols = slice(BANK * j, BANK * j + BANK)
-                bank = psum.tile([P, BANK], F32, tag="bank")
-                nc.tensor.matmul(
-                    out=bank[:], lhsT=ones[:], rhs=bias_row[:, cols], start=True, stop=True
-                )
-                nc.scalar.copy(out=bias_bc[:, cols], in_=bank[:])
 
         def turn_words(rows_bf16, turned_bf16):
             words = rows_bf16.bitcast(F32)
@@ -164,12 +150,10 @@ def tile_essattn_pb_kernel(tc, q_feat, kv, v, w_proj, b_proj, out):
             first_i = b * TILES + pair * PAIR
             return slice(first_i, first_i + PAIR)
 
-        def root(b, pair):
-            cols = pair_cols(b, pair)
+        def root(b, cols):
             nc.scalar.sqrt(out=norm[:, cols], in_=sumsq[:, cols])
 
-        def invert(b, pair):
-            cols = pair_cols(b, pair)
+        def invert(b, cols):
             nc.vector.tensor_scalar_max(out=floored[:, cols], in0=norm[:, cols], scalar1=EPS_NORM)
             nc.vector.reciprocal(out=rnorm[:, cols], in_=floored[:, cols])
 
@@ -199,37 +183,23 @@ def tile_essattn_pb_kernel(tc, q_feat, kv, v, w_proj, b_proj, out):
         def turn_values(b, j):
             turn_words(v_sb[b][:, j, :], v_turned[:, b * TILES + j])
 
-        def on_tensor(dst, src):
-            bank = psum.tile([P, BANK], F32, tag="bank")
-            values = bank[:].bitcast(BF16)
-            for half in range(2):
-                nc.tensor.matmul(
-                    out=values[:, BANK * half : BANK * half + BANK],
-                    lhsT=ident_bf[:],
-                    rhs=src[half],
-                    start=True,
-                    stop=True,
-                )
-            nc.scalar.copy(out=dst.rearrange("p n t -> p (n t)").bitcast(F32), in_=bank[:])
-
         def new_group():
             grouped = regroup_pool.tile([P, BANK, SLOTS], BF16, tag="grouped", align_bytes=64)
             return grouped
 
-        def regroup_state(grouped, b, c, g, hu, engine):
-            first = BANK * g + 256 * hu
-            rows = kv_sb[b][c][:, :, first : first + 256]
-            here = grouped[:, 256 * hu : 256 * hu + 256, :]
-            if engine == "tensor":
-                on_tensor(here, [rows[:, :, e::2].rearrange("p t m -> p m t") for e in range(2)])
-                return
-            src = rows.rearrange("p t (m i e) -> p e m t i", i=RUN, e=2)
-            dst = here.rearrange("p (e m i) t -> p e m t i", e=2, i=RUN)
-            if engine == "scalar":
-                for e in range(2):
-                    nc.scalar.copy(out=dst[:, e], in_=src[:, e])
-            else:
+        def regroup_state(grouped, b, c, g, on_scalar=()):
+            src = kv_sb[b][c][:, :, BANK * g : BANK * g + BANK].rearrange(
+                "p t (m i e) -> p e m t i", i=RUN, e=2
+            )
+            dst = grouped[:].rearrange("p (e m i) t -> p e m t i", e=2, i=RUN)
+            if not on_scalar:
                 nc.vector.tensor_copy(out=dst, in_=src)
+                return
+            for e in range(2):
+                if e in on_scalar:
+                    nc.scalar.copy(out=dst[:, e], in_=src[:, e])
+                else:
+                    nc.vector.tensor_copy(out=dst[:, e], in_=src[:, e])
 
         def quantise_state(grouped, b, c, g):
             cols = slice(BANK * g, BANK * g + BANK)
@@ -239,22 +209,16 @@ def tile_essattn_pb_kernel(tc, q_feat, kv, v, w_proj, b_proj, out):
                 in_=grouped[:].rearrange("p n t -> p (n t)"),
             )
 
-        def regroup_weights(grouped, g, j, hu, engine):
-            first = BANK * j + 256 * hu
-            rows = w_sb[g][:, :, first : first + 256]
-            here = grouped[:, 256 * hu : 256 * hu + 256, :]
-            if engine == "tensor":
-                on_tensor(
-                    here,
-                    [rows[:, :, P * e : P * e + P].rearrange("p t m -> p m t") for e in range(2)],
-                )
-                return
-            src = rows.rearrange("p t (m i) -> p m t i", i=RUN)
-            dst = here.rearrange("p (m i) t -> p m t i", i=RUN)
-            if engine == "scalar":
-                nc.scalar.copy(out=dst, in_=src)
-            else:
-                nc.vector.tensor_copy(out=dst, in_=src)
+        def regroup_weights(grouped, g, j, on_scalar=()):
+            src = w_sb[g][:, :, BANK * j : BANK * j + BANK].rearrange("p t (m i) -> p m t i", i=RUN)
+            dst = grouped[:].rearrange("p (m i) t -> p m t i", i=RUN)
+            steps = BANK // RUN
+            for e in range(2):
+                part = slice(steps // 2 * e, steps // 2 * e + steps // 2)
+                if e in on_scalar:
+                    nc.scalar.copy(out=dst[:, part], in_=src[:, part])
+                else:
+                    nc.vector.tensor_copy(out=dst[:, part], in_=src[:, part])
 
         def quantise_weights(grouped, g, j):
             cols = slice(BANK * j, BANK * j + BANK)
@@ -271,13 +235,17 @@ def tile_essattn_pb_kernel(tc, q_feat, kv, v, w_proj, b_proj, out):
                 in_=h_grouped[:].rearrange("p g r t -> p (g r t)"),
             )
 
-        def first_product(i):
-            b = i // TILES
+        def new_h():
             h_grouped = h_pool.tile([P, PASSES, P, SLOTS], BF16, align_bytes=64)
-            for g in range(PASSES):
+            return h_grouped
+
+        def first_product(h_grouped, i, halves=(0, 1)):
+            b = i // TILES
+            for g in halves:
                 t2_bank = psum.tile([P, SLOTS, P], F32, tag="bank")
                 for t in range(SLOTS):
-                    cols = slice(BANK * g + P * t, BANK * g + P * t + P)
+                    start_col = BANK * g + 256 * (t % 2) + P * (t // 2)
+                    cols = slice(start_col, start_col + P)
                     for c in range(PASSES):
                         nc.tensor.matmul_mx(
                             out=t2_bank[:, t, :],
@@ -296,7 +264,6 @@ def tile_essattn_pb_kernel(tc, q_feat, kv, v, w_proj, b_proj, out):
                     op0=ALU.mult,
                     op1=ALU.add,
                 )
-            return h_grouped
 
         def second_product(i, j, on_vector):
             cols = slice(BANK * j, BANK * j + BANK)
@@ -323,101 +290,101 @@ def tile_essattn_pb_kernel(tc, q_feat, kv, v, w_proj, b_proj, out):
                 )
             nc.sync.dma_start(out=out_rows[i * P : (i + 1) * P, cols], in_=result[:])
 
+        column_halves = range(OUT_COLS // BANK)
+        state = {}
+        weights = {}
+        h = {}
+
+        def regroup(b, c, g, on_scalar=()):
+            state[b, c, g] = new_group()
+            regroup_state(state[b, c, g], b, c, g, on_scalar)
+
+        def quant_state(b, c, g):
+            quantise_state(state[b, c, g], b, c, g)
+
+        def regroup_w(g, j, on_scalar=()):
+            weights[g, j] = new_group()
+            regroup_weights(weights[g, j], g, j, on_scalar)
+
+
         square(0, 0)
         square(0, 1, True)
-        root(0, 0)
-        invert(0, 0)
+        root(0, pair_cols(0, 0))
+        invert(0, pair_cols(0, 0))
         q2 = scale_queries(0, 0)
         turned = turn_queries(q2)
-        groups = [new_group() for g in range(PASSES)]
-        for g in range(PASSES):
-            for hu in range(HALVES):
-                regroup_state(groups[g], 0, 0, g, hu, "vector")
+        regroup(0, 0, 0)
         square(0, 2)
         square(0, 3)
-        root(0, 1)
+        root(0, pair_cols(0, 1))
         quantise_queries(0, 0, turned)
-        quantise_state(groups[0], 0, 0, 0)
-        quantise_state(groups[1], 0, 0, 1)
-        invert(0, 1)
-        groups = [new_group() for g in range(PASSES)]
-        regroup_state(groups[0], 0, 1, 0, 0, "vector")
+        regroup(0, 0, 1, (1,))
+        quant_state(0, 0, 0)
+        regroup(0, 1, 0, (1,))
+        invert(0, pair_cols(0, 1))
         q2 = scale_queries(0, 1)
-        regroup_state(groups[0], 0, 1, 0, 1, "tensor")
-        regroup_state(groups[1], 0, 1, 1, 1, "tensor")
-        regroup_state(groups[1], 0, 1, 1, 0, "scalar")
         turned = turn_queries(q2)
-        for g in range(PASSES):
-            quantise_state(groups[g], 0, 1, g)
+        quant_state(0, 1, 0)
+        regroup(0, 1, 1, (1,))
         quantise_queries(0, 1, turned)
-        for j in range(TILES):
-            turn_values(0, j)
-        wg = {(g, j): new_group() for g in range(2) for j in range(2)}
-        groups = [[new_group() for g in range(PASSES)] for c in range(PASSES)]
-        h = {}
-        h[0] = first_product(0)
-        for hu in range(HALVES):
-            regroup_weights(wg[0, 0], 0, 0, hu, "vector")
-        h[1] = first_product(1)
-        quantise_h(0, h[0])
-        square(1, 0)
-        square(1, 1)
-        root(1, 0)
-        spread_bias()
-        for hu in range(HALVES):
-            regroup_weights(wg[1, 0], 1, 0, hu, "tensor")
-        h[2] = first_product(2)
-        quantise_h(1, h[1])
-        invert(1, 0)
-        q2a = scale_queries(1, 0)
-        h[3] = first_product(3)
-        turned = turn_queries(q2a)
-        square(1, 2)
-        quantise_h(2, h[2])
-        for hu in range(HALVES):
-            regroup_weights(wg[0, 1], 0, 1, hu, "tensor")
-        regroup_state(groups[0][0], 1, 0, 0, 0, "vector")
-        quantise_weights(wg[0, 0], 0, 0)
+        quant_state(0, 0, 1)
+        for i in range(TILES):
+            turn_values(0, i)
+        for i in range(TILES):
+            h[i] = new_h()
+            if i == 1:
+                quant_state(0, 1, 1)
+            first_product(h[i], i, (0,))
+        regroup_w(0, 0, (0, 1))
+        for i in range(TILES):
+            square(1, i)
+            if i == PAIR:
+                root(1, pair_cols(1, 0))
+        root(1, pair_cols(1, 1))
+        for i in range(TILES):
+            first_product(h[i], i, (1,))
+            if i > 0:
+                quantise_h(i - 1, h[i - 1])
+        regroup_w(1, 0, (0, 1))
         quantise_h(3, h[3])
-        quantise_weights(wg[1, 0], 1, 0)
-        for hu in range(HALVES):
-            regroup_weights(wg[1, 1], 1, 1, hu, "tensor")
-        square(1, 3)
-        root(1, 1)
+        invert(1, pair_cols(1, 0))
+        q2 = scale_queries(1, 0)
+        turned = turn_queries(q2)
+        invert(1, pair_cols(1, 1))
+        q2 = scale_queries(1, 1)
+        turned_last = turn_queries(q2)
+        for g in range(PASSES):
+            quantise_weights(weights[g, 0], g, 0)
         quantise_queries(1, 0, turned)
+        regroup(1, 0, 0, (1,))
         for i in range(TILES):
             second_product(i, 0, True)
-        for g in range(2):
-            regroup_state(groups[0][g], 1, 0, g, 1, "tensor")
-        regroup_state(groups[0][1], 1, 0, 1, 0, "scalar")
-        invert(1, 1)
-        q2 = scale_queries(1, 1)
-        turned = turn_queries(q2)
-        regroup_state(groups[1][0], 1, 1, 0, 0, "vector")
-        regroup_state(groups[1][0], 1, 1, 0, 1, "tensor")
-        for g in range(PASSES):
-            quantise_weights(wg[g, 1], g, 1)
-        quantise_state(groups[0][0], 1, 0, 0)
-        quantise_state(groups[0][1], 1, 0, 1)
-        for hu in range(HALVES):
-            regroup_state(groups[1][1], 1, 1, 1, hu, "scalar")
+        quant_state(1, 0, 0)
+        regroup(1, 1, 0, (1,))
+        quantise_queries(1, 1, turned_last)
+        quant_state(1, 1, 0)
+        regroup(1, 0, 1, (1,))
+        regroup(1, 1, 1, (1,))
+        for i in range(TILES):
+            turn_values(1, i)
+        for i in range(TILES, ALL_TILES):
+            h[i] = new_h()
+            first_product(h[i], i, (0,))
+            if i == TILES:
+                quant_state(1, 0, 1)
+        quant_state(1, 1, 1)
+        regroup_w(0, 1, (0, 1))
+        regroup_w(1, 1, (0, 1))
+        for i in range(TILES, ALL_TILES):
+            first_product(h[i], i, (1,))
+            if i > TILES:
+                quantise_h(i - 1, h[i - 1])
+            if i == TILES + 2:
+                for g in range(PASSES):
+                    quantise_weights(weights[g, 1], g, 1)
+        quantise_h(ALL_TILES - 1, h[ALL_TILES - 1])
         for i in range(TILES):
             second_product(i, 1, True)
-        quantise_queries(1, 1, turned)
-        for j in range(TILES):
-            turn_values(1, j)
-        for g in range(2):
-            quantise_state(groups[1][g], 1, 1, g)
-        waiting = None
         for i in range(TILES, ALL_TILES):
-            h = first_product(i)
-            if waiting is not None:
-                quantise_h(*waiting)
-                if i > TILES + 1:
-                    for j in range(2):
-                        second_product(i - 2, j, True)
-            waiting = (i, h)
-        quantise_h(*waiting)
-        for i in range(ALL_TILES - 2, ALL_TILES):
             for j in range(2):
                 second_product(i, j, True)

@@ -41,7 +41,7 @@ def tile_essattn_pb_kernel(tc, q_feat, kv, v, w_proj, b_proj, out):
         keep = ctx.enter_context(tc.tile_pool(name="keep", bufs=1))
         scratch = ctx.enter_context(tc.tile_pool(name="scratch", bufs=2))
         regroup_pool = ctx.enter_context(tc.tile_pool(name="regroup", bufs=9))
-        h_pool = ctx.enter_context(tc.tile_pool(name="h", bufs=6))
+        h_pool = ctx.enter_context(tc.tile_pool(name="h", bufs=3))
         store_pool = ctx.enter_context(tc.tile_pool(name="store", bufs=8))
         psum = ctx.enter_context(tc.psum_pool(name="psum", bufs=8))
 
@@ -63,30 +63,42 @@ def tile_essattn_pb_kernel(tc, q_feat, kv, v, w_proj, b_proj, out):
         w_sb = [inputs.tile([P, SLOTS, OUT_COLS], BF16, name="w_sb%d" % g) for g in range(PASSES)]
         bias_bc = const.tile([P, OUT_COLS], BF16)
 
-        def load_queries_and_state(b):
+        def load_queries(b, pair):
+            tiles = slice(PAIR * pair, PAIR * pair + PAIR)
             q_rows = q_feat[b].rearrange("(i p) k -> p i k", p=P)
+            nc.sync.dma_start(out=q_sb[b][:, tiles, :], in_=q_rows[:, tiles, :])
+
+        def load_state(b, c):
             kv_rows = kv[b].rearrange(
                 "(c u p e) n -> c p u (e n)", c=PASSES, u=HALVES, p=P, e=2
             )
-            for c in range(PASSES):
-                pair = slice(PAIR * c, PAIR * c + PAIR)
-                nc.sync.dma_start(out=q_sb[b][:, pair, :], in_=q_rows[:, pair, :])
-                nc.sync.dma_start(
-                    out=kv_sb[b][c][:].rearrange("p (u e) n -> p u (e n)", u=HALVES),
-                    in_=kv_rows[c],
-                )
+            nc.sync.dma_start(
+                out=kv_sb[b][c][:].rearrange("p (u e) n -> p u (e n)", u=HALVES),
+                in_=kv_rows[c],
+            )
 
         def load_values(b):
-            nc.sync.dma_start(out=v_sb[b][:], in_=v[b].rearrange("(i p) n -> p i n", p=P))
+            v_rows = v[b].rearrange("(i p) n -> p i n", p=P)
+            for pair in range(PAIRS):
+                tiles = slice(PAIR * pair, PAIR * pair + PAIR)
+                nc.sync.dma_start(out=v_sb[b][:, tiles, :], in_=v_rows[:, tiles, :])
 
-        load_queries_and_state(0)
-        load_values(0)
         w_rows = w_proj.rearrange("(g u p e) n -> g p u (e n)", g=PASSES, u=HALVES, p=P, e=2)
-        for g in range(PASSES):
+
+        def load_weights(g):
             nc.sync.dma_start(
                 out=w_sb[g][:].rearrange("p (u e) n -> p u (e n)", u=HALVES), in_=w_rows[g]
             )
-        load_queries_and_state(1)
+
+        for c in range(PASSES):
+            load_queries(0, c)
+            load_state(0, c)
+        load_values(0)
+        for c in range(PASSES):
+            load_queries(1, c)
+            load_weights(c)
+        for c in range(PASSES):
+            load_state(1, c)
         load_values(1)
         nc.sync.dma_start(out=bias_bc[:], in_=b_proj.partition_broadcast(P))
 
@@ -228,20 +240,21 @@ def tile_essattn_pb_kernel(tc, q_feat, kv, v, w_proj, b_proj, out):
                 in_=grouped[:].rearrange("p n t -> p (n t)"),
             )
 
-        def quantise_h(i, h_grouped):
+        def quantise_h(i, h_pair):
+            tiles = slice(i, i + PAIR)
             nc.vector.quantize_mx(
-                out=h_codes[:, i].rearrange("p g r -> p (g r)").bitcast(FP8X4),
-                scales=h_scales[:, i].rearrange("p g r -> p (g r)"),
-                in_=h_grouped[:].rearrange("p g r t -> p (g r t)"),
+                out=h_codes[:, tiles].rearrange("p i g r -> p (i g r)").bitcast(FP8X4),
+                scales=h_scales[:, tiles].rearrange("p i g r -> p (i g r)"),
+                in_=h_pair[:].rearrange("p i g r t -> p (i g r t)"),
             )
 
         def new_h():
-            h_grouped = h_pool.tile([P, PASSES, P, SLOTS], BF16, align_bytes=64)
-            return h_grouped
+            h_pair = h_pool.tile([P, PAIR, PASSES, P, SLOTS], BF16, align_bytes=64)
+            return h_pair
 
-        def first_product(h_grouped, i, halves=(0, 1)):
+        def multiply(i, g):
             b = i // TILES
-            for g in halves:
+            if True:
                 t2_bank = psum.tile([P, SLOTS, P], F32, tag="bank")
                 for t in range(SLOTS):
                     start_col = BANK * g + 256 * (t % 2) + P * (t // 2)
@@ -256,14 +269,22 @@ def tile_essattn_pb_kernel(tc, q_feat, kv, v, w_proj, b_proj, out):
                             start=(c == 0),
                             stop=(c == PASSES - 1),
                         )
+            return t2_bank
+
+        def add_values(h_pair, i, g, t2_bank):
+            if True:
                 nc.vector.scalar_tensor_tensor(
-                    out=h_grouped[:, g],
+                    out=h_pair[:, i % PAIR, g],
                     in0=t2_bank[:].rearrange("p t r -> p r t"),
                     scalar=1.0 / math.sqrt(TOKENS),
                     in1=v_turned[:, i, g],
                     op0=ALU.mult,
                     op1=ALU.add,
                 )
+
+        def first_product(h_pair, i, halves=(0, 1)):
+            for g in halves:
+                add_values(h_pair, i, g, multiply(i, g))
 
         def second_product(i, j, on_vector):
             cols = slice(BANK * j, BANK * j + BANK)
@@ -306,7 +327,6 @@ def tile_essattn_pb_kernel(tc, q_feat, kv, v, w_proj, b_proj, out):
             weights[g, j] = new_group()
             regroup_weights(weights[g, j], g, j, on_scalar)
 
-
         square(0, 0)
         square(0, 1, True)
         root(0, pair_cols(0, 0))
@@ -314,39 +334,41 @@ def tile_essattn_pb_kernel(tc, q_feat, kv, v, w_proj, b_proj, out):
         q2 = scale_queries(0, 0)
         turned = turn_queries(q2)
         regroup(0, 0, 0)
-        square(0, 2)
-        square(0, 3)
-        root(0, pair_cols(0, 1))
         quantise_queries(0, 0, turned)
         regroup(0, 0, 1, (1,))
         quant_state(0, 0, 0)
         regroup(0, 1, 0, (1,))
-        invert(0, pair_cols(0, 1))
-        q2 = scale_queries(0, 1)
-        turned = turn_queries(q2)
+        square(0, 2)
+        square(0, 3)
+        root(0, pair_cols(0, 1))
         quant_state(0, 1, 0)
-        regroup(0, 1, 1, (1,))
-        quantise_queries(0, 1, turned)
-        quant_state(0, 0, 1)
         for i in range(TILES):
             turn_values(0, i)
-        for i in range(TILES):
-            h[i] = new_h()
-            if i == 1:
-                quant_state(0, 1, 1)
-            first_product(h[i], i, (0,))
+        h[0] = new_h()
+        banks = [multiply(i, 0) for i in range(PAIR)]
+        regroup(0, 1, 1, (1,))
+        quant_state(0, 0, 1)
+        for i in range(PAIR):
+            add_values(h[0], i, 0, banks[i])
+        invert(0, pair_cols(0, 1))
+        q2 = scale_queries(0, 1)
+        quant_state(0, 1, 1)
+        turned = turn_queries(q2)
+        for i in range(PAIR):
+            first_product(h[0], i, (1,))
+        quantise_queries(0, 1, turned)
+        quantise_h(0, h[0])
         regroup_w(0, 0, (0, 1))
         for i in range(TILES):
             square(1, i)
             if i == PAIR:
                 root(1, pair_cols(1, 0))
         root(1, pair_cols(1, 1))
-        for i in range(TILES):
-            first_product(h[i], i, (1,))
-            if i > 0:
-                quantise_h(i - 1, h[i - 1])
+        h[2] = new_h()
+        for i in range(PAIR, TILES):
+            first_product(h[2], i)
         regroup_w(1, 0, (0, 1))
-        quantise_h(3, h[3])
+        quantise_h(2, h[2])
         invert(1, pair_cols(1, 0))
         q2 = scale_queries(1, 0)
         turned = turn_queries(q2)
@@ -368,21 +390,22 @@ def tile_essattn_pb_kernel(tc, q_feat, kv, v, w_proj, b_proj, out):
         for i in range(TILES):
             turn_values(1, i)
         for i in range(TILES, ALL_TILES):
-            h[i] = new_h()
-            first_product(h[i], i, (0,))
+            if i % PAIR == 0:
+                h[i] = new_h()
+            first_product(h[i - i % PAIR], i, (0,))
             if i == TILES:
                 quant_state(1, 0, 1)
         quant_state(1, 1, 1)
         regroup_w(0, 1, (0, 1))
         regroup_w(1, 1, (0, 1))
         for i in range(TILES, ALL_TILES):
-            first_product(h[i], i, (1,))
-            if i > TILES:
-                quantise_h(i - 1, h[i - 1])
+            first_product(h[i - i % PAIR], i, (1,))
+            if i == TILES + PAIR:
+                quantise_h(TILES, h[TILES])
             if i == TILES + 2:
                 for g in range(PASSES):
                     quantise_weights(weights[g, 1], g, 1)
-        quantise_h(ALL_TILES - 1, h[ALL_TILES - 1])
+        quantise_h(ALL_TILES - PAIR, h[ALL_TILES - PAIR])
         for i in range(TILES):
             second_product(i, 1, True)
         for i in range(TILES, ALL_TILES):

@@ -65,7 +65,7 @@ def tile_essattn_pb_kernel(tc, q_feat, kv, v, w_proj, b_proj, out):
 
         def load_queries(b, pair):
             tiles = slice(PAIR * pair, PAIR * pair + PAIR)
-            q_rows = q_feat[b].rearrange("(i p) k -> p i k", p=P)
+            q_rows = q_feat[b].rearrange("(p i) k -> p i k", p=P)
             nc.sync.dma_start(out=q_sb[b][:, tiles, :], in_=q_rows[:, tiles, :])
 
         def load_state(b, c):
@@ -78,7 +78,7 @@ def tile_essattn_pb_kernel(tc, q_feat, kv, v, w_proj, b_proj, out):
             )
 
         def load_values(b):
-            v_rows = v[b].rearrange("(i p) n -> p i n", p=P)
+            v_rows = v[b].rearrange("(p i) n -> p i n", p=P)
             for pair in range(PAIRS):
                 tiles = slice(PAIR * pair, PAIR * pair + PAIR)
                 nc.sync.dma_start(out=v_sb[b][:, tiles, :], in_=v_rows[:, tiles, :])
@@ -122,7 +122,7 @@ def tile_essattn_pb_kernel(tc, q_feat, kv, v, w_proj, b_proj, out):
         floored = const.tile([P, ALL_TILES], F32)
         norm = const.tile([P, ALL_TILES], F32)
         rnorm = const.tile([P, ALL_TILES], F32)
-        out_rows = out.flatten_outer_dims()
+        out_rows = [out[b].rearrange("(p i) n -> p i n", p=P) for b in range(BATCH)]
 
         def turn_words(rows_bf16, turned_bf16):
             words = rows_bf16.bitcast(F32)
@@ -309,7 +309,7 @@ def tile_essattn_pb_kernel(tc, q_feat, kv, v, w_proj, b_proj, out):
                 nc.gpsimd.tensor_tensor(
                     out=result[:], in0=result[:], in1=bias_bc[:, cols], op=ALU.add
                 )
-            nc.sync.dma_start(out=out_rows[i * P : (i + 1) * P, cols], in_=result[:])
+            nc.sync.dma_start(out=out_rows[i // TILES][:, i % TILES, cols], in_=result[:])
 
         column_halves = range(OUT_COLS // BANK)
         state = {}

@@ -40,25 +40,33 @@ def tile_essattn_pb_kernel(tc, q_feat, kv, v, w_proj, b_proj, out):
         inputs = ctx.enter_context(tc.tile_pool(name="inputs", bufs=1))
         keep = ctx.enter_context(tc.tile_pool(name="keep", bufs=1))
         scratch = ctx.enter_context(tc.tile_pool(name="scratch", bufs=2))
-        regroup_pool = ctx.enter_context(tc.tile_pool(name="regroup", bufs=9))
+        regroup_pool = ctx.enter_context(tc.tile_pool(name="regroup", bufs=8))
         h_pool = ctx.enter_context(tc.tile_pool(name="h", bufs=3))
-        store_pool = ctx.enter_context(tc.tile_pool(name="store", bufs=8))
+        store_pool = ctx.enter_context(tc.tile_pool(name="store", bufs=7))
+        shared_pool = ctx.enter_context(tc.tile_pool(name="shared", bufs=TILES))
         psum = ctx.enter_context(tc.psum_pool(name="psum", bufs=8))
 
         one = const.tile([P, 1], F32)
         nc.vector.memset(one[:], 1.0)
         table_warm = const.tile([P, 1], F32)
-        nc.scalar.sqrt(out=table_warm[:], in_=one[:])
+        nc.scalar.activation(out=table_warm[:], in_=one[:], func=ACT.Square)
+        exponent = const.tile([P, PAIR], F32)
+        nc.gpsimd.memset(exponent[:], -0.5)
         ident = const.tile([P, P], F32)
         make_identity(nc, ident[:])
-        ident_bf = const.tile([P, P], BF16)
-        nc.vector.tensor_copy(out=ident_bf[:], in_=ident[:])
 
         q_sb = [inputs.tile([P, TILES, FEAT], BF16, name="q_sb%d" % b) for b in range(BATCH)]
         v_sb = [inputs.tile([P, TILES, FEAT], BF16, name="v_sb%d" % b) for b in range(BATCH)]
         kv_sb = [
-            [inputs.tile([P, SLOTS, FEAT], BF16, name="kv_sb%d%d" % (b, c)) for c in range(PASSES)]
+            {
+                c: inputs.tile([P, SLOTS, FEAT], BF16, name="kv_sb%d%d" % (b, c))
+                for c in range(PASSES)
+                if (b, c) != (0, 0)
+            }
             for b in range(BATCH)
+        ]
+        first_kv_sb = [
+            inputs.tile([P, SLOTS, BANK], BF16, name="first_kv_sb%d" % g) for g in range(FEAT // BANK)
         ]
         w_sb = [inputs.tile([P, SLOTS, OUT_COLS], BF16, name="w_sb%d" % g) for g in range(PASSES)]
         bias_bc = const.tile([P, OUT_COLS], BF16)
@@ -83,6 +91,16 @@ def tile_essattn_pb_kernel(tc, q_feat, kv, v, w_proj, b_proj, out):
                 tiles = slice(PAIR * pair, PAIR * pair + PAIR)
                 nc.sync.dma_start(out=v_sb[b][:, tiles, :], in_=v_rows[:, tiles, :])
 
+        def load_first_state(g):
+            kv_rows = kv[0].rearrange(
+                "(c u p e) n -> c u p e n", c=PASSES, u=HALVES, p=P, e=2
+            )
+            cols = slice(BANK * g, BANK * g + BANK)
+            for u in range(HALVES):
+                nc.sync.dma_start(
+                    out=first_kv_sb[g][:, 2 * u : 2 * u + 2, :], in_=kv_rows[0, u][:, :, cols]
+                )
+
         w_rows = w_proj.rearrange("(g u p e) n -> g p u (e n)", g=PASSES, u=HALVES, p=P, e=2)
 
         def load_weights(g):
@@ -90,9 +108,11 @@ def tile_essattn_pb_kernel(tc, q_feat, kv, v, w_proj, b_proj, out):
                 out=w_sb[g][:].rearrange("p (u e) n -> p u (e n)", u=HALVES), in_=w_rows[g]
             )
 
-        for c in range(PASSES):
-            load_queries(0, c)
-            load_state(0, c)
+        load_first_state(0)
+        load_queries(0, 0)
+        load_first_state(1)
+        load_queries(0, 1)
+        load_state(0, 1)
         load_values(0)
         for c in range(PASSES):
             load_queries(1, c)
@@ -120,7 +140,6 @@ def tile_essattn_pb_kernel(tc, q_feat, kv, v, w_proj, b_proj, out):
 
         sumsq = const.tile([P, ALL_TILES], F32)
         floored = const.tile([P, ALL_TILES], F32)
-        norm = const.tile([P, ALL_TILES], F32)
         rnorm = const.tile([P, ALL_TILES], F32)
         out_rows = [out[b].rearrange("(p i) n -> p i n", p=P) for b in range(BATCH)]
 
@@ -162,12 +181,13 @@ def tile_essattn_pb_kernel(tc, q_feat, kv, v, w_proj, b_proj, out):
             first_i = b * TILES + pair * PAIR
             return slice(first_i, first_i + PAIR)
 
-        def root(b, cols):
-            nc.scalar.sqrt(out=norm[:, cols], in_=sumsq[:, cols])
-
-        def invert(b, cols):
-            nc.vector.tensor_scalar_max(out=floored[:, cols], in0=norm[:, cols], scalar1=EPS_NORM)
-            nc.vector.reciprocal(out=rnorm[:, cols], in_=floored[:, cols])
+        def invert_norm(cols):
+            nc.gpsimd.tensor_scalar_max(
+                out=floored[:, cols], in0=sumsq[:, cols], scalar1=EPS_NORM * EPS_NORM
+            )
+            nc.gpsimd.tensor_tensor(
+                out=rnorm[:, cols], in0=floored[:, cols], in1=exponent[:], op=ALU.pow
+            )
 
         def scale_queries(b, pair):
             q2 = scratch.tile([P, PAIR, FEAT], BF16, tag="q2")
@@ -200,9 +220,11 @@ def tile_essattn_pb_kernel(tc, q_feat, kv, v, w_proj, b_proj, out):
             return grouped
 
         def regroup_state(grouped, b, c, g, on_scalar=()):
-            src = kv_sb[b][c][:, :, BANK * g : BANK * g + BANK].rearrange(
-                "p t (m i e) -> p e m t i", i=RUN, e=2
-            )
+            if (b, c) == (0, 0):
+                rows = first_kv_sb[g][:]
+            else:
+                rows = kv_sb[b][c][:, :, BANK * g : BANK * g + BANK]
+            src = rows.rearrange("p t (m i e) -> p e m t i", i=RUN, e=2)
             dst = grouped[:].rearrange("p (e m i) t -> p e m t i", e=2, i=RUN)
             if not on_scalar:
                 nc.vector.tensor_copy(out=dst, in_=src)
@@ -286,7 +308,7 @@ def tile_essattn_pb_kernel(tc, q_feat, kv, v, w_proj, b_proj, out):
             for g in halves:
                 add_values(h_pair, i, g, multiply(i, g))
 
-        def second_product(i, j, on_vector):
+        def multiply_h(i, j):
             cols = slice(BANK * j, BANK * j + BANK)
             out_bank = psum.tile([P, BANK], F32, tag="bank")
             for g in range(PASSES):
@@ -299,17 +321,31 @@ def tile_essattn_pb_kernel(tc, q_feat, kv, v, w_proj, b_proj, out):
                     start=(g == 0),
                     stop=(g == PASSES - 1),
                 )
-            result = store_pool.tile([P, BANK], F32)
-            if on_vector:
-                nc.vector.tensor_tensor(
-                    out=result[:], in0=out_bank[:], in1=bias_bc[:, cols], op=ALU.add
-                )
-            else:
-                nc.scalar.copy(out=result[:], in_=out_bank[:])
-                nc.gpsimd.tensor_tensor(
-                    out=result[:], in0=result[:], in1=bias_bc[:, cols], op=ALU.add
-                )
-            nc.sync.dma_start(out=out_rows[i // TILES][:, i % TILES, cols], in_=result[:])
+            return out_bank
+
+        def store(queue, i, j, result):
+            cols = slice(BANK * j, BANK * j + BANK)
+            queue.dma_start(out=out_rows[i // TILES][:, i % TILES, cols], in_=result[:])
+
+        def leave(out_bank, i, j):
+            cols = slice(BANK * j, BANK * j + BANK)
+            result = store_pool.tile([P, BANK], F32, tag="by_vector")
+            nc.vector.tensor_tensor(
+                out=result[:], in0=out_bank[:], in1=bias_bc[:, cols], op=ALU.add
+            )
+            store(nc.sync, i, j, result)
+
+        def share(out_bank, i, j):
+            cols = slice(BANK * j, BANK * j + BANK)
+            result = shared_pool.tile([P, BANK], F32, tag="by_scalar")
+            nc.scalar.copy(out=result[:], in_=out_bank[:])
+            nc.gpsimd.tensor_tensor(
+                out=result[:], in0=result[:], in1=bias_bc[:, cols], op=ALU.add
+            )
+            return result
+
+        def second_product(i, j):
+            leave(multiply_h(i, j), i, j)
 
         column_halves = range(OUT_COLS // BANK)
         state = {}
@@ -327,87 +363,99 @@ def tile_essattn_pb_kernel(tc, q_feat, kv, v, w_proj, b_proj, out):
             weights[g, j] = new_group()
             regroup_weights(weights[g, j], g, j, on_scalar)
 
-        square(0, 0)
-        square(0, 1, True)
-        root(0, pair_cols(0, 0))
-        invert(0, pair_cols(0, 0))
-        q2 = scale_queries(0, 0)
-        turned = turn_queries(q2)
-        regroup(0, 0, 0)
-        quantise_queries(0, 0, turned)
-        regroup(0, 0, 1, (1,))
-        quant_state(0, 0, 0)
-        regroup(0, 1, 0, (1,))
-        square(0, 2)
-        square(0, 3)
-        root(0, pair_cols(0, 1))
-        quant_state(0, 1, 0)
-        for i in range(TILES):
-            turn_values(0, i)
-        h[0] = new_h()
-        banks = [multiply(i, 0) for i in range(PAIR)]
-        regroup(0, 1, 1, (1,))
-        quant_state(0, 0, 1)
-        for i in range(PAIR):
-            add_values(h[0], i, 0, banks[i])
-        invert(0, pair_cols(0, 1))
-        q2 = scale_queries(0, 1)
-        quant_state(0, 1, 1)
-        turned = turn_queries(q2)
-        for i in range(PAIR):
-            first_product(h[0], i, (1,))
-        quantise_queries(0, 1, turned)
-        quantise_h(0, h[0])
-        regroup_w(0, 0, (0, 1))
-        for i in range(TILES):
-            square(1, i)
-            if i == PAIR:
-                root(1, pair_cols(1, 0))
-        root(1, pair_cols(1, 1))
-        h[2] = new_h()
-        for i in range(PAIR, TILES):
-            first_product(h[2], i)
-        regroup_w(1, 0, (0, 1))
-        quantise_h(2, h[2])
-        invert(1, pair_cols(1, 0))
-        q2 = scale_queries(1, 0)
-        turned = turn_queries(q2)
-        invert(1, pair_cols(1, 1))
-        q2 = scale_queries(1, 1)
-        turned_last = turn_queries(q2)
-        for g in range(PASSES):
-            quantise_weights(weights[g, 0], g, 0)
-        quantise_queries(1, 0, turned)
-        regroup(1, 0, 0, (1,))
-        for i in range(TILES):
-            second_product(i, 0, True)
-        quant_state(1, 0, 0)
-        regroup(1, 1, 0, (1,))
-        quantise_queries(1, 1, turned_last)
-        quant_state(1, 1, 0)
-        regroup(1, 0, 1, (1,))
-        regroup(1, 1, 1, (1,))
-        for i in range(TILES):
-            turn_values(1, i)
-        for i in range(TILES, ALL_TILES):
-            if i % PAIR == 0:
-                h[i] = new_h()
-            first_product(h[i - i % PAIR], i, (0,))
-            if i == TILES:
-                quant_state(1, 0, 1)
-        quant_state(1, 1, 1)
-        regroup_w(0, 1, (0, 1))
-        regroup_w(1, 1, (0, 1))
-        for i in range(TILES, ALL_TILES):
-            first_product(h[i - i % PAIR], i, (1,))
-            if i == TILES + PAIR:
-                quantise_h(TILES, h[TILES])
-            if i == TILES + 2:
-                for g in range(PASSES):
-                    quantise_weights(weights[g, 1], g, 1)
-        quantise_h(ALL_TILES - PAIR, h[ALL_TILES - PAIR])
-        for i in range(TILES):
-            second_product(i, 1, True)
-        for i in range(TILES, ALL_TILES):
-            for j in range(2):
-                second_product(i, j, True)
+        engines = {mybir.EngineType.DVE, mybir.EngineType.Activation, mybir.EngineType.PE}
+        with tc.manual_schedule(engines=engines):
+            regroup(0, 0, 0)
+            square(0, 0)
+            square(0, 1, True)
+            quant_state(0, 0, 0)
+            invert_norm(pair_cols(0, 0))
+            regroup(0, 0, 1)
+            square(0, 2)
+            square(0, 3)
+            invert_norm(pair_cols(0, 1))
+            q2 = scale_queries(0, 0)
+            turned = turn_queries(q2)
+            quant_state(0, 0, 1)
+            regroup(0, 1, 0)
+            q2 = scale_queries(0, 1)
+            quantise_queries(0, 0, turned)
+            for i in range(PAIR):
+                turn_values(0, i)
+            turned = turn_queries(q2)
+            quant_state(0, 1, 0)
+            h[0] = new_h()
+            banks = [multiply(i, 0) for i in range(PAIR)]
+            regroup(0, 1, 1)
+            square(1, 0)
+            for i in range(PAIR, TILES):
+                turn_values(0, i)
+            quant_state(0, 1, 1)
+            quantise_queries(0, 1, turned)
+            for i in range(PAIR):
+                add_values(h[0], i, 0, banks[i])
+            for i in range(PAIR):
+                first_product(h[0], i, (1,))
+            h[2] = new_h()
+            first_product(h[2], 2, (0,))
+            quantise_h(0, h[0])
+            first_product(h[2], 2, (1,))
+            first_product(h[2], 3)
+            square(1, 1)
+            invert_norm(pair_cols(1, 0))
+            square(1, 2)
+            square(1, 3)
+            invert_norm(pair_cols(1, 1))
+            regroup_w(0, 0, (0, 1))
+            q2 = scale_queries(1, 0)
+            quantise_h(2, h[2])
+            regroup(1, 0, 0)
+            quantise_weights(weights[0, 0], 0, 0)
+            regroup_w(1, 0, (0, 1))
+            turned = turn_queries(q2)
+            q2 = scale_queries(1, 1)
+            quant_state(1, 0, 0)
+            turn_values(1, 0)
+            turn_values(1, 1)
+            turned_last = turn_queries(q2)
+            turn_values(1, 2)
+            turn_values(1, 3)
+            regroup(1, 1, 0)
+            quantise_queries(1, 0, turned)
+            quant_state(1, 1, 0)
+            h[4] = new_h()
+            banks = [multiply(i, 0) for i in (4, 5)]
+            quantise_weights(weights[1, 0], 1, 0)
+            regroup(1, 0, 1, (1,))
+            quantise_queries(1, 1, turned_last)
+            for i in (4, 5):
+                add_values(h[4], i, 0, banks[i - 4])
+            h[6] = new_h()
+            for i in (6, 7):
+                first_product(h[6], i, (0,))
+            quant_state(1, 0, 1)
+            regroup(1, 1, 1, (1,))
+            for g in range(PASSES):
+                regroup_w(g, 1, (0, 1))
+            second_product(0, 0)
+            early = [multiply_h(i, 0) for i in (1, 2, 3)]
+            quant_state(1, 1, 1)
+            banks = [multiply(i, 1) for i in range(TILES, ALL_TILES)]
+            leave(early[0], 1, 0)
+            store(nc.scalar, 3, 0, share(early[2], 3, 0))
+            quantise_weights(weights[0, 1], 0, 1)
+            leave(early[1], 2, 0)
+            for i in (4, 5):
+                add_values(h[4], i, 1, banks[i - TILES])
+            quantise_weights(weights[1, 1], 1, 1)
+            add_values(h[6], 6, 1, banks[2])
+            quantise_h(4, h[4])
+            add_values(h[6], 7, 1, banks[3])
+            second_product(3, 1)
+            quantise_h(6, h[6])
+            shared = [(i, 1, share(multiply_h(i, 1), i, 1)) for i in (0, 1, 2)]
+            for i in range(TILES, ALL_TILES):
+                for j in range(2):
+                    second_product(i, j)
+            for i, j, result in shared:
+                store(nc.scalar, i, j, result)

@@ -49,9 +49,7 @@ def tile_essattn_pb_kernel(tc, q_feat, kv, v, w_proj, b_proj, out):
         one = const.tile([P, 1], F32)
         nc.vector.memset(one[:], 1.0)
         table_warm = const.tile([P, 1], F32)
-        nc.scalar.activation(out=table_warm[:], in_=one[:], func=ACT.Square)
-        exponent = const.tile([P, PAIR], F32)
-        nc.gpsimd.memset(exponent[:], -0.5)
+        nc.scalar.sqrt(out=table_warm[:], in_=one[:])
         ident = const.tile([P, P], F32)
         make_identity(nc, ident[:])
 
@@ -140,6 +138,7 @@ def tile_essattn_pb_kernel(tc, q_feat, kv, v, w_proj, b_proj, out):
 
         sumsq = const.tile([P, ALL_TILES], F32)
         floored = const.tile([P, ALL_TILES], F32)
+        norm = const.tile([P, ALL_TILES], F32)
         rnorm = const.tile([P, ALL_TILES], F32)
         out_rows = [out[b].rearrange("(p i) n -> p i n", p=P) for b in range(BATCH)]
 
@@ -181,13 +180,14 @@ def tile_essattn_pb_kernel(tc, q_feat, kv, v, w_proj, b_proj, out):
             first_i = b * TILES + pair * PAIR
             return slice(first_i, first_i + PAIR)
 
+        def root(cols):
+            nc.scalar.sqrt(out=norm[:, cols], in_=sumsq[:, cols])
+
+        def floor_norm(cols):
+            nc.vector.tensor_scalar_max(out=floored[:, cols], in0=norm[:, cols], scalar1=EPS_NORM)
+
         def invert_norm(cols):
-            nc.gpsimd.tensor_scalar_max(
-                out=floored[:, cols], in0=sumsq[:, cols], scalar1=EPS_NORM * EPS_NORM
-            )
-            nc.gpsimd.tensor_tensor(
-                out=rnorm[:, cols], in0=floored[:, cols], in1=exponent[:], op=ALU.pow
-            )
+            nc.vector.reciprocal(out=rnorm[:, cols], in_=floored[:, cols])
 
         def scale_queries(b, pair):
             q2 = scratch.tile([P, PAIR, FEAT], BF16, tag="q2")
@@ -368,16 +368,20 @@ def tile_essattn_pb_kernel(tc, q_feat, kv, v, w_proj, b_proj, out):
             regroup(0, 0, 0)
             square(0, 0)
             square(0, 1, True)
+            root(pair_cols(0, 0))
             quant_state(0, 0, 0)
+            floor_norm(pair_cols(0, 0))
             invert_norm(pair_cols(0, 0))
             regroup(0, 0, 1)
             square(0, 2)
             square(0, 3)
-            invert_norm(pair_cols(0, 1))
+            root(pair_cols(0, 1))
             q2 = scale_queries(0, 0)
             turned = turn_queries(q2)
             quant_state(0, 0, 1)
+            floor_norm(pair_cols(0, 1))
             regroup(0, 1, 0)
+            invert_norm(pair_cols(0, 1))
             q2 = scale_queries(0, 1)
             quantise_queries(0, 0, turned)
             for i in range(PAIR):
@@ -388,6 +392,7 @@ def tile_essattn_pb_kernel(tc, q_feat, kv, v, w_proj, b_proj, out):
             banks = [multiply(i, 0) for i in range(PAIR)]
             regroup(0, 1, 1)
             square(1, 0)
+            square(1, 1)
             for i in range(PAIR, TILES):
                 turn_values(0, i)
             quant_state(0, 1, 1)
@@ -400,19 +405,23 @@ def tile_essattn_pb_kernel(tc, q_feat, kv, v, w_proj, b_proj, out):
             first_product(h[2], 2, (0,))
             quantise_h(0, h[0])
             first_product(h[2], 2, (1,))
-            first_product(h[2], 3)
-            square(1, 1)
+            root(pair_cols(1, 0))
+            floor_norm(pair_cols(1, 0))
+            first_product(h[2], 3, (0,))
             invert_norm(pair_cols(1, 0))
+            first_product(h[2], 3, (1,))
             square(1, 2)
             square(1, 3)
-            invert_norm(pair_cols(1, 1))
+            root(pair_cols(1, 1))
             regroup_w(0, 0, (0, 1))
             q2 = scale_queries(1, 0)
             quantise_h(2, h[2])
+            floor_norm(pair_cols(1, 1))
             regroup(1, 0, 0)
+            invert_norm(pair_cols(1, 1))
             quantise_weights(weights[0, 0], 0, 0)
-            regroup_w(1, 0, (0, 1))
             turned = turn_queries(q2)
+            regroup_w(1, 0, (0, 1))
             q2 = scale_queries(1, 1)
             quant_state(1, 0, 0)
             turn_values(1, 0)

import math
from contextlib import ExitStack

import concourse.mybir as mybir
from concourse.masks import make_identity

BF16 = mybir.dt.bfloat16
F32 = mybir.dt.float32
U32 = mybir.dt.uint32
U8 = mybir.dt.uint8
FP8X4 = mybir.dt.float8_e4m3fn_x4
ALU = mybir.AluOpType
ACT = mybir.ActivationFunctionType

P = 128
BATCH = 2
TOKENS = 512
FEAT = 1024
OUT_COLS = 1024
EPS_NORM = 1e-12

SLOTS = 4
HALVES = 2
PASSES = FEAT // (P * SLOTS)
TILES = TOKENS // P
ALL_TILES = BATCH * TILES
BANK = 512

PAIR = 2
PAIRS = TILES // PAIR
RUN = 4

FLOPS = 2 * BATCH * TOKENS * FEAT * FEAT + 2 * BATCH * TOKENS * FEAT * OUT_COLS


def tile_essattn_pb_kernel(tc, q_feat, kv, v, w_proj, b_proj, out):
    nc = tc.nc
    with ExitStack() as ctx:
        const = ctx.enter_context(tc.tile_pool(name="const", bufs=1))
        inputs = ctx.enter_context(tc.tile_pool(name="inputs", bufs=1))
        keep = ctx.enter_context(tc.tile_pool(name="keep", bufs=1))
        scratch = ctx.enter_context(tc.tile_pool(name="scratch", bufs=2))
        regroup_pool = ctx.enter_context(tc.tile_pool(name="regroup", bufs=8))
        h_pool = ctx.enter_context(tc.tile_pool(name="h", bufs=3))
        store_pool = ctx.enter_context(tc.tile_pool(name="store", bufs=7))
        shared_pool = ctx.enter_context(tc.tile_pool(name="shared", bufs=TILES))
        psum = ctx.enter_context(tc.psum_pool(name="psum", bufs=8))

        one = const.tile([P, 1], F32)
        nc.vector.memset(one[:], 1.0)
        table_warm = const.tile([P, 1], F32)
        nc.scalar.sqrt(out=table_warm[:], in_=one[:])
        ident = const.tile([P, P], F32)
        make_identity(nc, ident[:])

        q_sb = [inputs.tile([P, TILES, FEAT], BF16, name="q_sb%d" % b) for b in range(BATCH)]
        v_sb = [inputs.tile([P, TILES, FEAT], BF16, name="v_sb%d" % b) for b in range(BATCH)]
        kv_sb = [
            {
                c: inputs.tile([P, SLOTS, FEAT], BF16, name="kv_sb%d%d" % (b, c))
                for c in range(PASSES)
                if (b, c) != (0, 0)
            }
            for b in range(BATCH)
        ]
        first_kv_sb = [
            inputs.tile([P, SLOTS, BANK], BF16, name="first_kv_sb%d" % g) for g in range(FEAT // BANK)
        ]
        w_sb = [inputs.tile([P, SLOTS, OUT_COLS], BF16, name="w_sb%d" % g) for g in range(PASSES)]
        bias_bc = const.tile([P, OUT_COLS], BF16)

        def load_queries(b, pair):
            tiles = slice(PAIR * pair, PAIR * pair + PAIR)
            q_rows = q_feat[b].rearrange("(p i) k -> p i k", p=P)
            nc.sync.dma_start(out=q_sb[b][:, tiles, :], in_=q_rows[:, tiles, :])

        def load_state(b, c):
            kv_rows = kv[b].rearrange(
                "(c u p e) n -> c p u (e n)", c=PASSES, u=HALVES, p=P, e=2
            )
            nc.sync.dma_start(
                out=kv_sb[b][c][:].rearrange("p (u e) n -> p u (e n)", u=HALVES),
                in_=kv_rows[c],
            )

        def load_values(b):
            v_rows = v[b].rearrange("(p i) n -> p i n", p=P)
            for pair in range(PAIRS):
                tiles = slice(PAIR * pair, PAIR * pair + PAIR)
                nc.sync.dma_start(out=v_sb[b][:, tiles, :], in_=v_rows[:, tiles, :])

        def load_first_state(g):
            kv_rows = kv[0].rearrange(
                "(c u p e) n -> c u p e n", c=PASSES, u=HALVES, p=P, e=2
            )
            cols = slice(BANK * g, BANK * g + BANK)
            for u in range(HALVES):
                nc.sync.dma_start(
                    out=first_kv_sb[g][:, 2 * u : 2 * u + 2, :], in_=kv_rows[0, u][:, :, cols]
                )

        w_rows = w_proj.rearrange("(g u p e) n -> g p u (e n)", g=PASSES, u=HALVES, p=P, e=2)

        def load_weights(g):
            nc.sync.dma_start(
                out=w_sb[g][:].rearrange("p (u e) n -> p u (e n)", u=HALVES), in_=w_rows[g]
            )

        load_first_state(0)
        load_queries(0, 0)
        load_first_state(1)
        load_queries(0, 1)
        load_state(0, 1)
        load_values(0)
        for c in range(PASSES):
            load_queries(1, c)
            load_weights(c)
        for c in range(PASSES):
            load_state(1, c)
        load_values(1)
        nc.sync.dma_start(out=bias_bc[:], in_=b_proj.partition_broadcast(P))

        q2_codes = keep.tile([P, ALL_TILES, PASSES, P], U32, align_bytes=64)
        q2_scales = keep.tile([P, ALL_TILES, PASSES, P], U8, align_bytes=64)
        kv_codes = [
            keep.tile([P, PASSES, FEAT], U32, name="kv_codes%d" % b, align_bytes=64)
            for b in range(BATCH)
        ]
        kv_scales = [
            keep.tile([P, PASSES, FEAT], U8, name="kv_scales%d" % b, align_bytes=64)
            for b in range(BATCH)
        ]
        h_codes = keep.tile([P, ALL_TILES, PASSES, P], U32, align_bytes=64)
        h_scales = keep.tile([P, ALL_TILES, PASSES, P], U8, align_bytes=64)
        w_codes = keep.tile([P, PASSES, OUT_COLS], U32, align_bytes=64)
        w_scales = keep.tile([P, PASSES, OUT_COLS], U8, align_bytes=64)
        v_turned = keep.tile([P, ALL_TILES, PASSES, P, SLOTS], BF16)

        sumsq = const.tile([P, ALL_TILES], F32)
        floored = const.tile([P, ALL_TILES], F32)
        norm = const.tile([P, ALL_TILES], F32)
        rnorm = const.tile([P, ALL_TILES], F32)
        out_rows = [out[b].rearrange("(p i) n -> p i n", p=P) for b in range(BATCH)]

        def turn_words(rows_bf16, turned_bf16):
            words = rows_bf16.bitcast(F32)
            bank = psum.tile([P, PASSES, HALVES, P], F32, tag="bank")
            for c in range(PASSES):
                for u in range(HALVES):
                    first = (c * HALVES + u) * P
                    nc.tensor.transpose(
                        out=bank[:, c, u, :], in_=words[:, first : first + P], identity=ident[:]
                    )
            nc.scalar.copy(
                out=turned_bf16.bitcast(F32), in_=bank[:].rearrange("p c u r -> p c r u")
            )

        def square(b, j, on_vector=False):
            i = b * TILES + j
            squares = scratch.tile([P, FEAT], BF16, tag="squares")
            if on_vector:
                nc.vector.scalar_tensor_tensor(
                    out=squares[:],
                    in0=q_sb[b][:, j, :],
                    scalar=1.0,
                    in1=q_sb[b][:, j, :],
                    op0=ALU.mult,
                    op1=ALU.mult,
                    accum_out=sumsq[:, i : i + 1],
                )
                return
            nc.scalar.activation(
                out=squares[:],
                in_=q_sb[b][:, j, :],
                func=ACT.Square,
                accum_out=sumsq[:, i : i + 1],
            )

        def pair_cols(b, pair):
            first_i = b * TILES + pair * PAIR
            return slice(first_i, first_i + PAIR)

        def root(cols):
            nc.scalar.sqrt(out=norm[:, cols], in_=sumsq[:, cols])

        def floor_norm(cols):
            nc.vector.tensor_scalar_max(out=floored[:, cols], in0=norm[:, cols], scalar1=EPS_NORM)

        def invert_norm(cols):
            nc.vector.reciprocal(out=rnorm[:, cols], in_=floored[:, cols])

        def scale_queries(b, pair):
            q2 = scratch.tile([P, PAIR, FEAT], BF16, tag="q2")
            for k in range(PAIR):
                i = b * TILES + pair * PAIR + k
                nc.vector.tensor_scalar_mul(
                    out=q2[:, k, :], in0=q_sb[b][:, pair * PAIR + k, :], scalar1=rnorm[:, i : i + 1]
                )
            return q2

        def turn_queries(q2):
            q2_turned = scratch.tile([P, PAIR, PASSES, P, SLOTS], BF16, tag="turned", align_bytes=64)
            for k in range(PAIR):
                turn_words(q2[:, k, :], q2_turned[:, k])
            return q2_turned

        def quantise_queries(b, pair, q2_turned):
            cols = pair_cols(b, pair)
            nc.vector.quantize_mx(
                out=q2_codes[:, cols].rearrange("p i c r -> p (i c r)").bitcast(FP8X4),
                scales=q2_scales[:, cols].rearrange("p i c r -> p (i c r)"),
                in_=q2_turned[:].rearrange("p i c r t -> p (i c r t)"),
            )

        def turn_values(b, j):
            turn_words(v_sb[b][:, j, :], v_turned[:, b * TILES + j])

        def new_group():
            grouped = regroup_pool.tile([P, BANK, SLOTS], BF16, tag="grouped", align_bytes=64)
            return grouped

        def regroup_state(grouped, b, c, g, on_scalar=()):
            if (b, c) == (0, 0):
                rows = first_kv_sb[g][:]
            else:
                rows = kv_sb[b][c][:, :, BANK * g : BANK * g + BANK]
            src = rows.rearrange("p t (m i e) -> p e m t i", i=RUN, e=2)
            dst = grouped[:].rearrange("p (e m i) t -> p e m t i", e=2, i=RUN)
            if not on_scalar:
                nc.vector.tensor_copy(out=dst, in_=src)
                return
            for e in range(2):
                if e in on_scalar:
                    nc.scalar.copy(out=dst[:, e], in_=src[:, e])
                else:
                    nc.vector.tensor_copy(out=dst[:, e], in_=src[:, e])

        def quantise_state(grouped, b, c, g):
            cols = slice(BANK * g, BANK * g + BANK)
            nc.vector.quantize_mx(
                out=kv_codes[b][:, c, cols].bitcast(FP8X4),
                scales=kv_scales[b][:, c, cols],
                in_=grouped[:].rearrange("p n t -> p (n t)"),
            )

        def regroup_weights(grouped, g, j, on_scalar=()):
            src = w_sb[g][:, :, BANK * j : BANK * j + BANK].rearrange("p t (m i) -> p m t i", i=RUN)
            dst = grouped[:].rearrange("p (m i) t -> p m t i", i=RUN)
            steps = BANK // RUN
            for e in range(2):
                part = slice(steps // 2 * e, steps // 2 * e + steps // 2)
                if e in on_scalar:
                    nc.scalar.copy(out=dst[:, part], in_=src[:, part])
                else:
                    nc.vector.tensor_copy(out=dst[:, part], in_=src[:, part])

        def quantise_weights(grouped, g, j):
            cols = slice(BANK * j, BANK * j + BANK)
            nc.vector.quantize_mx(
                out=w_codes[:, g, cols].bitcast(FP8X4),
                scales=w_scales[:, g, cols],
                in_=grouped[:].rearrange("p n t -> p (n t)"),
            )

        def quantise_h(i, h_pair):
            tiles = slice(i, i + PAIR)
            nc.vector.quantize_mx(
                out=h_codes[:, tiles].rearrange("p i g r -> p (i g r)").bitcast(FP8X4),
                scales=h_scales[:, tiles].rearrange("p i g r -> p (i g r)"),
                in_=h_pair[:].rearrange("p i g r t -> p (i g r t)"),
            )

        def new_h():
            h_pair = h_pool.tile([P, PAIR, PASSES, P, SLOTS], BF16, align_bytes=64)
            return h_pair

        def multiply(i, g):
            b = i // TILES
            if True:
                t2_bank = psum.tile([P, SLOTS, P], F32, tag="bank")
                for t in range(SLOTS):
                    start_col = BANK * g + 256 * (t % 2) + P * (t // 2)
                    cols = slice(start_col, start_col + P)
                    for c in range(PASSES):
                        nc.tensor.matmul_mx(
                            out=t2_bank[:, t, :],
                            lhsT=kv_codes[b][:, c, cols].bitcast(FP8X4),
                            lhsT_scale=kv_scales[b][:, c, cols],
                            rhs=q2_codes[:, i, c, :].bitcast(FP8X4),
                            rhs_scale=q2_scales[:, i, c, :],
                            start=(c == 0),
                            stop=(c == PASSES - 1),
                        )
            return t2_bank

        def add_values(h_pair, i, g, t2_bank):
            if True:
                nc.vector.scalar_tensor_tensor(
                    out=h_pair[:, i % PAIR, g],
                    in0=t2_bank[:].rearrange("p t r -> p r t"),
                    scalar=1.0 / math.sqrt(TOKENS),
                    in1=v_turned[:, i, g],
                    op0=ALU.mult,
                    op1=ALU.add,
                )

        def first_product(h_pair, i, halves=(0, 1)):
            for g in halves:
                add_values(h_pair, i, g, multiply(i, g))

        def multiply_h(i, j):
            cols = slice(BANK * j, BANK * j + BANK)
            out_bank = psum.tile([P, BANK], F32, tag="bank")
            for g in range(PASSES):
                nc.tensor.matmul_mx(
                    out=out_bank[:],
                    lhsT=h_codes[:, i, g, :].bitcast(FP8X4),
                    lhsT_scale=h_scales[:, i, g, :],
                    rhs=w_codes[:, g, cols].bitcast(FP8X4),
                    rhs_scale=w_scales[:, g, cols],
                    start=(g == 0),
                    stop=(g == PASSES - 1),
                )
            return out_bank

        def store(queue, i, j, result):
            cols = slice(BANK * j, BANK * j + BANK)
            queue.dma_start(out=out_rows[i // TILES][:, i % TILES, cols], in_=result[:])

        def leave(out_bank, i, j):
            cols = slice(BANK * j, BANK * j + BANK)
            result = store_pool.tile([P, BANK], F32, tag="by_vector")
            nc.vector.tensor_tensor(
                out=result[:], in0=out_bank[:], in1=bias_bc[:, cols], op=ALU.add
            )
            store(nc.sync, i, j, result)

        def share(out_bank, i, j):
            cols = slice(BANK * j, BANK * j + BANK)
            result = shared_pool.tile([P, BANK], F32, tag="by_scalar")
            nc.scalar.copy(out=result[:], in_=out_bank[:])
            nc.gpsimd.tensor_tensor(
                out=result[:], in0=result[:], in1=bias_bc[:, cols], op=ALU.add
            )
            return result

        def second_product(i, j):
            leave(multiply_h(i, j), i, j)

        column_halves = range(OUT_COLS // BANK)
        state = {}
        weights = {}
        h = {}

        def regroup(b, c, g, on_scalar=()):
            state[b, c, g] = new_group()
            regroup_state(state[b, c, g], b, c, g, on_scalar)

        def quant_state(b, c, g):
            quantise_state(state[b, c, g], b, c, g)

        def regroup_w(g, j, on_scalar=()):
            weights[g, j] = new_group()
            regroup_weights(weights[g, j], g, j, on_scalar)

        engines = {mybir.EngineType.DVE, mybir.EngineType.Activation, mybir.EngineType.PE}
        with tc.manual_schedule(engines=engines):
            regroup(0, 0, 0)
            square(0, 0)
            square(0, 1, True)
            root(pair_cols(0, 0))
            quant_state(0, 0, 0)
            floor_norm(pair_cols(0, 0))
            invert_norm(pair_cols(0, 0))
            regroup(0, 0, 1)
            square(0, 2)
            square(0, 3)
            root(pair_cols(0, 1))
            q2 = scale_queries(0, 0)
            turned = turn_queries(q2)
            quant_state(0, 0, 1)
            floor_norm(pair_cols(0, 1))
            regroup(0, 1, 0)
            invert_norm(pair_cols(0, 1))
            q2 = scale_queries(0, 1)
            quantise_queries(0, 0, turned)
            for i in range(PAIR):
                turn_values(0, i)
            turned = turn_queries(q2)
            quant_state(0, 1, 0)
            h[0] = new_h()
            banks = [multiply(i, 0) for i in range(PAIR)]
            regroup(0, 1, 1)
            square(1, 0)
            square(1, 1)
            for i in range(PAIR, TILES):
                turn_values(0, i)
            quant_state(0, 1, 1)
            quantise_queries(0, 1, turned)
            for i in range(PAIR):
                add_values(h[0], i, 0, banks[i])
            for i in range(PAIR):
                first_product(h[0], i, (1,))
            h[2] = new_h()
            first_product(h[2], 2, (0,))
            quantise_h(0, h[0])
            first_product(h[2], 2, (1,))
            root(pair_cols(1, 0))
            floor_norm(pair_cols(1, 0))
            first_product(h[2], 3, (0,))
            invert_norm(pair_cols(1, 0))
            first_product(h[2], 3, (1,))
            square(1, 2)
            square(1, 3)
            root(pair_cols(1, 1))
            regroup_w(0, 0, (0, 1))
            q2 = scale_queries(1, 0)
            quantise_h(2, h[2])
            floor_norm(pair_cols(1, 1))
            regroup(1, 0, 0)
            invert_norm(pair_cols(1, 1))
            quantise_weights(weights[0, 0], 0, 0)
            turned = turn_queries(q2)
            regroup_w(1, 0, (0, 1))
            q2 = scale_queries(1, 1)
            quant_state(1, 0, 0)
            turn_values(1, 0)
            turn_values(1, 1)
            turned_last = turn_queries(q2)
            turn_values(1, 2)
            turn_values(1, 3)
            regroup(1, 1, 0)
            quantise_queries(1, 0, turned)
            quant_state(1, 1, 0)
            h[4] = new_h()
            banks = [multiply(i, 0) for i in (4, 5)]
            quantise_weights(weights[1, 0], 1, 0)
            regroup(1, 0, 1, (1,))
            quantise_queries(1, 1, turned_last)
            for i in (4, 5):
                add_values(h[4], i, 0, banks[i - 4])
            h[6] = new_h()
            for i in (6, 7):
                first_product(h[6], i, (0,))
            quant_state(1, 0, 1)
            regroup(1, 1, 1, (1,))
            for g in range(PASSES):
                regroup_w(g, 1, (0, 1))
            second_product(0, 0)
            early = [multiply_h(i, 0) for i in (1, 2, 3)]
            quant_state(1, 1, 1)
            banks = [multiply(i, 1) for i in range(TILES, ALL_TILES)]
            leave(early[0], 1, 0)
            store(nc.scalar, 3, 0, share(early[2], 3, 0))
            quantise_weights(weights[0, 1], 0, 1)
            leave(early[1], 2, 0)
            for i in (4, 5):
                add_values(h[4], i, 1, banks[i - TILES])
            quantise_weights(weights[1, 1], 1, 1)
            add_values(h[6], 6, 1, banks[2])
            quantise_h(4, h[4])
            add_values(h[6], 7, 1, banks[3])
            second_product(3, 1)
            quantise_h(6, h[6])
            shared = [(i, 1, share(multiply_h(i, 1), i, 1)) for i in (0, 1, 2)]
            for i in range(TILES, ALL_TILES):
                for j in range(2):
                    second_product(i, j)
            for i, j, result in shared:
                store(nc.scalar, i, j, result)
